import numpy as np
import ml_dtypes


def mxq(x, axis, fmt="e4m3"):
    dtype, down = {"e4m3": (ml_dtypes.float8_e4m3fn, 7), "e5m2": (ml_dtypes.float8_e5m2, 14)}[fmt]
    v = np.moveaxis(np.asarray(x, np.float32).astype(ml_dtypes.bfloat16).astype(np.float64), axis, -1)
    blocks = v.reshape(v.shape[:-1] + (-1, 32))
    amax = np.abs(blocks).max(-1, keepdims=True)
    byte = np.maximum(np.where(amax > 0, np.frexp(amax)[1] - 1 + 127, 0) - down, 1)
    scale = np.exp2(byte - 127.0)
    codes = (blocks / scale).astype(np.float32).astype(dtype).astype(np.float64)
    return np.moveaxis((codes * scale).reshape(v.shape), -1, axis)


WIDE = False


def mx_kscale(k):
    if not WIDE:
        return np.ones(k)
    levels = np.array([10, -10, 5, -5, 0])
    a = np.random.permutation(np.resize(levels, k // 512 * 4)).reshape(k // 512, 4)
    idx = np.arange(k)
    return np.exp2(a[idx // 512, idx % 128 // 32])


BF16 = ml_dtypes.bfloat16


def bf(x):
    return np.asarray(x, np.float32).astype(BF16)


def f64(x):
    return np.asarray(x).astype(np.float64)


B, L = 2048, 512
PREDICT_GAP = 0.1
RELATION_GAP = 0.05


def setup_inputs():
    s = mx_kscale(L)
    up = s / s.min()
    dn = s.max() / s
    dens = 0.5 * (2.0 / L) ** np.random.random((B, 1))
    on = np.random.random((B, L)) < dens
    u = np.random.random((B, L))
    return {"predicts": bf(np.where(on, (0.62 + 0.36 * u) * up[None, :], 0.58 * u)),
            "adjList": bf(np.random.random((L, L)) * dn[:, None]),
            "label_prob_vec": bf(np.random.random(L))}


def reference(predicts, adjList, label_prob_vec):
    p, a, lp = f64(predicts), f64(adjList), f64(label_prob_vec)
    E = (p > 0.5 + PREDICT_GAP).astype(np.float64)
    offdiag = ~np.eye(L, dtype=bool)
    incr = ((a > lp[None, :] + RELATION_GAP) & offdiag).astype(np.float64)
    decr = ((a < lp[None, :] - RELATION_GAP) & offdiag).astype(np.float64)
    Ep = E * p
    Eq = mxq(E, 1, "e4m3")
    Epq = mxq(Ep, 1, "e4m3")
    num = (p
           + (Epq @ mxq(incr * a, 0, "e4m3"))
           + (Eq @ mxq(decr, 0, "e4m3"))
           - (Epq @ mxq(decr * (1.0 - a), 0, "e4m3")))
    rel = 1.0 + (E.sum(-1, keepdims=True) - E)
    return num / rel

@@ -1,0 +1,193 @@
+from contextlib import ExitStack
+
+import concourse.mybir as mybir
+from concourse.masks import make_identity
+
+F32 = mybir.dt.float32
+BF16 = mybir.dt.bfloat16
+U32 = mybir.dt.uint32
+U8 = mybir.dt.uint8
+FP8X4 = mybir.dt.float8_e4m3fn_x4
+ALU = mybir.AluOpType
+ACT = mybir.ActivationFunctionType
+
+P = 128
+B = 2048
+L = 512
+NT = B // P
+GT = 4
+NG = NT // GT
+FLOPS = 3 * 2 * B * L * L
+
+
+def tile_labelsmoothloss_pa_kernel(tc, predicts, adjList, label_prob_vec, out):
+    nc = tc.nc
+    with ExitStack() as ctx:
+        keep = ctx.enter_context(tc.tile_pool(name="keep", bufs=1))
+        grp = ctx.enter_context(tc.tile_pool(name="grp", bufs=2))
+        work = ctx.enter_context(tc.tile_pool(name="work", bufs=3))
+        ps_t = ctx.enter_context(tc.psum_pool(name="ps_t", bufs=2))
+        ps_a = ctx.enter_context(tc.psum_pool(name="ps_a", bufs=6))
+        ctx.enter_context(tc.manual_schedule())
+
+        lpb = keep.tile([P, L], BF16, name="lpb")
+        nc.scalar.dma_start(out=lpb[:], in_=label_prob_vec.partition_broadcast(P))
+        a_sb = keep.tile([P, 4 * L], BF16, name="a_sb")
+        nc.sync.dma_start(
+            out=a_sb[:].rearrange("q (u w) -> q u w", u=2),
+            in_=adjList.rearrange("(u q e) j -> q u (e j)", u=2, e=2),
+        )
+        p_sb = keep.tile([P, NT * L], BF16, name="p_sb")
+        p_dram = predicts.rearrange("(x r) j -> x (r j)", r=NT)
+        out_dram = out.rearrange("(x r) j -> x (r j)", r=NT)
+        for g in range(NG):
+            cols = slice(g * GT * L, (g + 1) * GT * L)
+            nc.sync.dma_start(out=p_sb[:, cols], in_=p_dram[:, cols])
+
+        ident = keep.tile([P, P], F32, name="ident")
+        make_identity(nc, ident[:])
+        moff = keep.tile([P, 4 * L], BF16, name="moff")
+        nc.vector.memset(moff[:], 1.0)
+        ioff = keep.tile([P, P], BF16, name="ioff")
+        nc.vector.tensor_scalar(out=ioff[:], in0=ident[:], scalar1=-1.0, scalar2=1.0, op0=ALU.mult, op1=ALU.add)
+        moff_v = moff[:].rearrange("q (t u c e) -> q t u c e", t=4, u=2, e=2)
+        for t in range(4):
+            nc.vector.tensor_copy(out=moff_v[:, t, t // 2, :, t % 2], in_=ioff[:])
+
+        sgn = keep.tile([P, NT * L], BF16, name="sgn")
+        ssum = keep.tile([P, NT], F32, name="ssum")
+        p_words = p_sb[:].bitcast(F32)
+        pt_gs = []
+        for g in range(NG):
+            pt_g = grp.tile([P, GT * L], BF16, name="pt_g", bufs=NG, align_bytes=64)
+            pt_gs.append(pt_g)
+            pt_gw = pt_g[:].bitcast(F32)
+            for h in range(GT // 2):
+                bank = ps_t.tile([P, 512], F32, name="bank")
+                for k in range(4):
+                    r = g * GT + h * 2 + k // 2
+                    u = k % 2
+                    nc.tensor.transpose(
+                        bank[:, k * P : (k + 1) * P],
+                        p_words[:, r * 256 + u * P : r * 256 + (u + 1) * P],
+                        ident[:],
+                    )
+                nc.scalar.copy(
+                    out=pt_gw[:, h * 512 : (h + 1) * 512].rearrange("q (r x u) -> q r x u", r=2, u=2),
+                    in_=bank[:].rearrange("q (r u x) -> q r x u", r=2, u=2),
+                )
+            for r in range(g * GT, (g + 1) * GT):
+                nc.scalar.activation(
+                    out=sgn[:, r * L : (r + 1) * L],
+                    in_=p_sb[:, r * L : (r + 1) * L],
+                    func=ACT.Sign,
+                    bias=-0.6,
+                    scale=1.0,
+                    accum_out=ssum[:, r : r + 1],
+                )
+
+        lp_m = keep.tile([P, 4 * L], BF16, name="lp_m")
+        nc.vector.tensor_tensor(
+            out=lp_m[:].rearrange("q (t j) -> q t j", t=4),
+            in0=moff[:].rearrange("q (t j) -> q t j", t=4),
+            in1=lpb[:].unsqueeze(1).to_broadcast([P, 4, L]),
+            op=ALU.mult,
+        )
+        a_m = keep.tile([P, 4 * L], BF16, name="a_m")
+        nc.vector.tensor_tensor(out=a_m[:], in0=a_sb[:], in1=moff[:], op=ALU.mult)
+        d_n = keep.tile([P, 4 * L], F32, name="d_n")
+        nc.vector.tensor_tensor(out=d_n[:], in0=a_m[:], in1=lp_m[:], op=ALU.subtract)
+        a_perm = a_m[:].rearrange("q (t j) -> q j t", t=4)
+        d_perm = d_n[:].rearrange("q (t j) -> q j t", t=4)
+
+        w_bf = [keep.tile([P, 4 * L], BF16, name="w_bf%d" % i, align_bytes=64) for i in range(3)]
+        w_c = [keep.tile([P, L], U32, name="w_c%d" % i, align_bytes=64) for i in range(3)]
+        w_s = [keep.tile([P, L], U8, name="w_s%d" % i, align_bytes=64) for i in range(3)]
+        wv = [w[:].rearrange("q (j t) -> q j t", t=4) for w in w_bf]
+
+        def quantise_w(i):
+            nc.vector.quantize_mx(out=w_c[i][:].bitcast(FP8X4), scales=w_s[i][:], in_=w_bf[i][:])
+
+        nc.vector.scalar_tensor_tensor(out=wv[0], in0=d_perm, scalar=0.05, in1=a_perm, op0=ALU.is_gt, op1=ALU.mult)
+        nc.vector.tensor_scalar(out=wv[1], in0=d_perm, scalar1=-0.05, scalar2=None, op0=ALU.is_lt)
+        quantise_w(0)
+        nc.vector.scalar_tensor_tensor(out=wv[2], in0=a_perm, scalar=1.0, in1=wv[1], op0=ALU.subtract, op1=ALU.mult)
+        quantise_w(1)
+
+        e_c = keep.tile([P, NT * P], U32, name="e_c", align_bytes=64)
+        e_s = keep.tile([P, NT * P], U8, name="e_s", align_bytes=64)
+        ep_c = keep.tile([P, NT * P], U32, name="ep_c", align_bytes=64)
+        ep_s = keep.tile([P, NT * P], U8, name="ep_s", align_bytes=64)
+        prev = None
+        for g in range(NG):
+            wcols = slice(g * GT * P, (g + 1) * GT * P)
+            et_g = grp.tile([P, GT * L], BF16, name="et_g", align_bytes=64)
+            ept_g = grp.tile([P, GT * L], BF16, name="ept_g", align_bytes=64)
+            nc.vector.tensor_scalar(out=et_g[:], in0=pt_gs[g][:], scalar1=0.6, scalar2=None, op0=ALU.is_gt)
+            if g == 0:
+                quantise_w(2)
+            else:
+                nc.vector.quantize_mx(out=ep_c[:, prev[0]].bitcast(FP8X4), scales=ep_s[:, prev[0]], in_=prev[1][:])
+            nc.vector.tensor_tensor(out=ept_g[:], in0=et_g[:], in1=pt_gs[g][:], op=ALU.mult)
+            nc.vector.quantize_mx(out=e_c[:, wcols].bitcast(FP8X4), scales=e_s[:, wcols], in_=et_g[:])
+            prev = (wcols, ept_g)
+
+        den = keep.tile([P, 2 * NT], F32, name="den")
+        rec = keep.tile([P, 2 * NT], F32, name="rec")
+        dif = keep.tile([P, NT], F32, name="dif")
+        hd = keep.tile([P, NT], F32, name="hd")
+        fm = keep.tile([P, NT], F32, name="fm")
+        nc.vector.tensor_scalar(out=den[:, 0:NT], in0=ssum[:], scalar1=0.5, scalar2=0.5 * L + 1.0, op0=ALU.mult, op1=ALU.add)
+        nc.vector.quantize_mx(out=ep_c[:, prev[0]].bitcast(FP8X4), scales=ep_s[:, prev[0]], in_=prev[1][:])
+        nc.vector.tensor_scalar(out=den[:, NT : 2 * NT], in0=den[:, 0:NT], scalar1=-1.0, scalar2=1.0, op0=ALU.add, op1=ALU.max)
+        nc.vector.reciprocal(out=rec[:], in_=den[:])
+        nc.vector.tensor_tensor(out=dif[:], in0=rec[:, NT : 2 * NT], in1=rec[:, 0:NT], op=ALU.subtract)
+        nc.vector.tensor_scalar(out=hd[:], in0=dif[:], scalar1=0.5, scalar2=None, op0=ALU.mult)
+        nc.vector.scalar_tensor_tensor(out=fm[:], in0=dif[:], scalar=0.5, in1=rec[:, 0:NT], op0=ALU.mult, op1=ALU.add)
+
+        NP = NT // 2
+        f_ts = [None] * NP
+        u_ts = [None] * NP
+
+        def products_and_add(r2):
+            f_t = work.tile([P, 2 * L], F32, name="f_t", bufs=NP)
+            u_t = work.tile([P, 2 * L], F32, name="u_t")
+            f_ts[r2] = f_t
+            u_ts[r2] = u_t
+            for k in range(2):
+                r = r2 * 2 + k
+                mcols = slice(r * P, (r + 1) * P)
+                acc = ps_a.tile([P, L], F32, name="acc")
+                ops = [(ep_c, ep_s, 0), (e_c, e_s, 1), (ep_c, ep_s, 2)]
+                for n, (c, s, i) in enumerate(ops):
+                    nc.tensor.matmul_mx(
+                        out=acc[:],
+                        lhsT=c[:, mcols].bitcast(FP8X4),
+                        lhsT_scale=s[:, mcols],
+                        rhs=w_c[i][:].bitcast(FP8X4),
+                        rhs_scale=w_s[i][:],
+                        start=(n == 0),
+                        stop=(n == 2),
+                    )
+                nc.scalar.activation(
+                    out=f_t[:, k * L : (k + 1) * L],
+                    in_=sgn[:, r * L : (r + 1) * L],
+                    func=ACT.Identity,
+                    bias=fm[:, r : r + 1],
+                    scale=hd[:, r : r + 1],
+                )
+                nc.vector.tensor_tensor(out=u_t[:, k * L : (k + 1) * L], in0=acc[:], in1=p_sb[:, r * L : (r + 1) * L], op=ALU.add)
+
+        def scale_and_store(r2, pieces):
+            o_t = work.tile([P, 2 * L], F32, name="o_t")
+            w = 2 * L // pieces
+            for k in range(pieces):
+                c = slice(k * w, (k + 1) * w)
+                nc.vector.tensor_tensor(out=o_t[:, c], in0=u_ts[r2][:, c], in1=f_ts[r2][:, c], op=ALU.mult)
+                nc.sync.dma_start(out=out_dram[:, r2 * 2 * L + k * w : r2 * 2 * L + (k + 1) * w], in_=o_t[:, c])
+
+        products_and_add(0)
+        for r2 in range(1, NP):
+            products_and_add(r2)
+            scale_and_store(r2 - 1, 1)
+        scale_and_store(NP - 1, 2)

@@ -17,6 +17,8 @@ L = 512
 NT = B // P
 GT = 4
 NG = NT // GT
+NP = NT // 2
+HB = NT // 2
 FLOPS = 3 * 2 * B * L * L
 
 
@@ -30,37 +32,46 @@ def tile_labelsmoothloss_pa_kernel(tc, predicts, adjList, label_prob_vec, out):
         ps_a = ctx.enter_context(tc.psum_pool(name="ps_a", bufs=6))
         ctx.enter_context(tc.manual_schedule())
 
-        lpb = keep.tile([P, L], BF16, name="lpb")
-        nc.scalar.dma_start(out=lpb[:], in_=label_prob_vec.partition_broadcast(P))
-        a_sb = keep.tile([P, 4 * L], BF16, name="a_sb")
-        nc.sync.dma_start(
-            out=a_sb[:].rearrange("q (u w) -> q u w", u=2),
-            in_=adjList.rearrange("(u q e) j -> q u (e j)", u=2, e=2),
-        )
+        lp_rows = keep.tile([P, P], BF16, name="lp_rows")
+        nc.vector.memset(lp_rows[:], 0.0)
+        nc.scalar.dma_start(out=lp_rows[0:4, :], in_=label_prob_vec.rearrange("(c p) -> c p", p=P))
         p_sb = keep.tile([P, NT * L], BF16, name="p_sb")
         p_dram = predicts.rearrange("(x r) j -> x (r j)", r=NT)
         out_dram = out.rearrange("(x r) j -> x (r j)", r=NT)
-        for g in range(NG):
-            cols = slice(g * GT * L, (g + 1) * GT * L)
+
+        def load_p(first, tiles):
+            cols = slice(first * L, (first + tiles) * L)
             nc.sync.dma_start(out=p_sb[:, cols], in_=p_dram[:, cols])
+
+        load_p(0, 2)
+        load_p(2, 2)
+        a_n = keep.tile([P, 4 * L], BF16, name="a_n")
+        nc.sync.dma_start(
+            out=a_n[:].rearrange("p (c j) -> p c j", c=4),
+            in_=adjList.rearrange("(c p) j -> p c j", p=P),
+        )
+        load_p(GT, GT)
+        a_q = keep.tile([P, 4 * L], BF16, name="a_q")
+        nc.sync.dma_start(
+            out=a_q[:].rearrange("q (u w) -> q u w", u=2),
+            in_=adjList.rearrange("(u q e) j -> q u (e j)", u=2, e=2),
+        )
+        for g in range(2, NG):
+            load_p(g * GT, GT)
 
         ident = keep.tile([P, P], F32, name="ident")
         make_identity(nc, ident[:])
-        moff = keep.tile([P, 4 * L], BF16, name="moff")
-        nc.vector.memset(moff[:], 1.0)
+        ident_b = keep.tile([P, P], BF16, name="ident_b")
+        make_identity(nc, ident_b[:])
         ioff = keep.tile([P, P], BF16, name="ioff")
         nc.vector.tensor_scalar(out=ioff[:], in0=ident[:], scalar1=-1.0, scalar2=1.0, op0=ALU.mult, op1=ALU.add)
-        moff_v = moff[:].rearrange("q (t u c e) -> q t u c e", t=4, u=2, e=2)
-        for t in range(4):
-            nc.vector.tensor_copy(out=moff_v[:, t, t // 2, :, t % 2], in_=ioff[:])
 
-        sgn = keep.tile([P, NT * L], BF16, name="sgn")
-        ssum = keep.tile([P, NT], F32, name="ssum")
         p_words = p_sb[:].bitcast(F32)
-        pt_gs = []
-        for g in range(NG):
+        pt_gs = [None] * NG
+
+        def transpose_p(g):
             pt_g = grp.tile([P, GT * L], BF16, name="pt_g", bufs=NG, align_bytes=64)
-            pt_gs.append(pt_g)
+            pt_gs[g] = pt_g
             pt_gw = pt_g[:].bitcast(F32)
             for h in range(GT // 2):
                 bank = ps_t.tile([P, 512], F32, name="bank")
@@ -76,88 +87,179 @@ def tile_labelsmoothloss_pa_kernel(tc, predicts, adjList, label_prob_vec, out):
                     out=pt_gw[:, h * 512 : (h + 1) * 512].rearrange("q (r x u) -> q r x u", r=2, u=2),
                     in_=bank[:].rearrange("q (r u x) -> q r x u", r=2, u=2),
                 )
-            for r in range(g * GT, (g + 1) * GT):
-                nc.scalar.activation(
-                    out=sgn[:, r * L : (r + 1) * L],
-                    in_=p_sb[:, r * L : (r + 1) * L],
-                    func=ACT.Sign,
-                    bias=-0.6,
-                    scale=1.0,
-                    accum_out=ssum[:, r : r + 1],
-                )
-
-        lp_m = keep.tile([P, 4 * L], BF16, name="lp_m")
-        nc.vector.tensor_tensor(
-            out=lp_m[:].rearrange("q (t j) -> q t j", t=4),
-            in0=moff[:].rearrange("q (t j) -> q t j", t=4),
-            in1=lpb[:].unsqueeze(1).to_broadcast([P, 4, L]),
-            op=ALU.mult,
-        )
-        a_m = keep.tile([P, 4 * L], BF16, name="a_m")
-        nc.vector.tensor_tensor(out=a_m[:], in0=a_sb[:], in1=moff[:], op=ALU.mult)
-        d_n = keep.tile([P, 4 * L], F32, name="d_n")
-        nc.vector.tensor_tensor(out=d_n[:], in0=a_m[:], in1=lp_m[:], op=ALU.subtract)
-        a_perm = a_m[:].rearrange("q (t j) -> q j t", t=4)
-        d_perm = d_n[:].rearrange("q (t j) -> q j t", t=4)
-
-        w_bf = [keep.tile([P, 4 * L], BF16, name="w_bf%d" % i, align_bytes=64) for i in range(3)]
-        w_c = [keep.tile([P, L], U32, name="w_c%d" % i, align_bytes=64) for i in range(3)]
-        w_s = [keep.tile([P, L], U8, name="w_s%d" % i, align_bytes=64) for i in range(3)]
-        wv = [w[:].rearrange("q (j t) -> q j t", t=4) for w in w_bf]
-
-        def quantise_w(i):
-            nc.vector.quantize_mx(out=w_c[i][:].bitcast(FP8X4), scales=w_s[i][:], in_=w_bf[i][:])
-
-        nc.vector.scalar_tensor_tensor(out=wv[0], in0=d_perm, scalar=0.05, in1=a_perm, op0=ALU.is_gt, op1=ALU.mult)
-        nc.vector.tensor_scalar(out=wv[1], in0=d_perm, scalar1=-0.05, scalar2=None, op0=ALU.is_lt)
-        quantise_w(0)
-        nc.vector.scalar_tensor_tensor(out=wv[2], in0=a_perm, scalar=1.0, in1=wv[1], op0=ALU.subtract, op1=ALU.mult)
-        quantise_w(1)
 
         e_c = keep.tile([P, NT * P], U32, name="e_c", align_bytes=64)
         e_s = keep.tile([P, NT * P], U8, name="e_s", align_bytes=64)
         ep_c = keep.tile([P, NT * P], U32, name="ep_c", align_bytes=64)
         ep_s = keep.tile([P, NT * P], U8, name="ep_s", align_bytes=64)
-        prev = None
-        for g in range(NG):
-            wcols = slice(g * GT * P, (g + 1) * GT * P)
-            et_g = grp.tile([P, GT * L], BF16, name="et_g", align_bytes=64)
-            ept_g = grp.tile([P, GT * L], BF16, name="ept_g", align_bytes=64)
-            nc.vector.tensor_scalar(out=et_g[:], in0=pt_gs[g][:], scalar1=0.6, scalar2=None, op0=ALU.is_gt)
-            if g == 0:
-                quantise_w(2)
-            else:
-                nc.vector.quantize_mx(out=ep_c[:, prev[0]].bitcast(FP8X4), scales=ep_s[:, prev[0]], in_=prev[1][:])
-            nc.vector.tensor_tensor(out=ept_g[:], in0=et_g[:], in1=pt_gs[g][:], op=ALU.mult)
-            nc.vector.quantize_mx(out=e_c[:, wcols].bitcast(FP8X4), scales=e_s[:, wcols], in_=et_g[:])
-            prev = (wcols, ept_g)
+        et_gs = [None] * NG
+        ept_gs = [None] * NG
 
+        WHOLE = slice(0, GT * L)
+
+        def make_e(g, c=WHOLE):
+            if et_gs[g] is None:
+                et_gs[g] = grp.tile([P, GT * L], BF16, name="et_g", align_bytes=64)
+            nc.vector.tensor_scalar(out=et_gs[g][:, c], in0=pt_gs[g][:, c], scalar1=0.6, scalar2=None, op0=ALU.is_gt)
+
+        def make_ep(g, c=WHOLE):
+            if ept_gs[g] is None:
+                ept_gs[g] = grp.tile([P, GT * L], BF16, name="ept_g", align_bytes=64)
+            nc.vector.tensor_tensor(out=ept_gs[g][:, c], in0=et_gs[g][:, c], in1=pt_gs[g][:, c], op=ALU.mult)
+
+        def quantise_e(g):
+            wcols = slice(g * GT * P, (g + 1) * GT * P)
+            nc.vector.quantize_mx(out=e_c[:, wcols].bitcast(FP8X4), scales=e_s[:, wcols], in_=et_gs[g][:])
+
+        def quantise_ep(g):
+            wcols = slice(g * GT * P, (g + 1) * GT * P)
+            nc.vector.quantize_mx(out=ep_c[:, wcols].bitcast(FP8X4), scales=ep_s[:, wcols], in_=ept_gs[g][:])
+
+        w_bf = [keep.tile([P, 4 * L], BF16, name="w_bf%d" % i, align_bytes=64) for i in range(3)]
+        w_c = [keep.tile([P, L], U32, name="w_c%d" % i, align_bytes=64) for i in range(3)]
+        w_s = [keep.tile([P, L], U8, name="w_s%d" % i, align_bytes=64) for i in range(3)]
+
+        def quantise_w(i):
+            nc.vector.quantize_mx(out=w_c[i][:].bitcast(FP8X4), scales=w_s[i][:], in_=w_bf[i][:])
+
+        def transpose_back(src, i):
+            src_w = src[:, 0 : 4 * L].bitcast(F32)
+            dst_w = w_bf[i][:].bitcast(F32)
+            for b in range(2):
+                wb = ps_a.tile([P, 512], F32, name="wb", tag="acc")
+                for cc in range(2):
+                    for u in range(2):
+                        nc.tensor.transpose(
+                            wb[:, u * 256 + cc * P : u * 256 + (cc + 1) * P],
+                            src_w[:, (2 * b + cc) * 256 + u * P : (2 * b + cc) * 256 + (u + 1) * P],
+                            ident[:],
+                        )
+                nc.scalar.copy(
+                    out=dst_w[:, b * 512 : (b + 1) * 512].rearrange("q (j u) -> q j u", u=2),
+                    in_=wb[:].rearrange("q (u j) -> q j u", u=2),
+                )
+
+        transpose_p(0)
+        lp_t = ps_a.tile([P, P], BF16, name="lp_t", tag="acc")
+        nc.tensor.transpose(lp_t[:], lp_rows[:], ident_b[:])
+        at_sb = keep.tile([P, 4 * L], BF16, name="at_sb")
+        for b in range(2):
+            at_ps = ps_a.tile([P, 2 * L], BF16, name="at_ps", tag="acc")
+            for cc in range(2):
+                for c in range(4):
+                    nc.tensor.transpose(
+                        at_ps[:, cc * L + c * P : cc * L + (c + 1) * P],
+                        a_n[:, c * L + (2 * b + cc) * P : c * L + (2 * b + cc + 1) * P],
+                        ident_b[:],
+                    )
+            nc.scalar.copy(out=at_sb[:, b * 2 * L : (b + 1) * 2 * L], in_=at_ps[:])
+        transpose_p(1)
+        am1_g = keep.tile([P, 4 * L], BF16, name="am1_g")
+        nc.scalar.activation(
+            out=am1_g[:].rearrange("q (j t) -> q j t", t=4),
+            in_=a_q[:].rearrange("q (t j) -> q j t", t=4),
+            func=ACT.Identity,
+            bias=-1.0,
+            scale=1.0,
+        )
+
+        for h in range(2):
+            make_e(0, slice(h * 2 * L, (h + 1) * 2 * L))
+            make_ep(0, slice(h * 2 * L, (h + 1) * 2 * L))
+        th_hi = keep.tile([P, 4], F32, name="th_hi")
+        th_lo = keep.tile([P, 4], F32, name="th_lo")
+        nc.vector.tensor_scalar(out=th_hi[:], in0=lp_t[:, 0:4], scalar1=0.05, scalar2=None, op0=ALU.add)
+        nc.vector.tensor_scalar(out=th_lo[:], in0=lp_t[:, 0:4], scalar1=-0.05, scalar2=None, op0=ALU.add)
+        quantise_e(0)
+        quantise_ep(0)
+
+        incr_t = keep.tile([P, 4 * L], BF16, name="incr_t")
+        w1_t = keep.tile([P, 4 * 640], BF16, name="w1_t")
+        w2_t = keep.tile([P, 4 * 640], BF16, name="w2_t")
+        ioff_b = ioff[:].unsqueeze(1).to_broadcast([P, 4, P])
+        for cj in range(4):
+            c = slice(cj * L, (cj + 1) * L)
+            nc.vector.tensor_scalar(out=w2_t[:, c], in0=at_sb[:, c], scalar1=th_lo[:, cj : cj + 1], scalar2=None, op0=ALU.is_lt)
+        for cj in range(4):
+            c = slice(cj * L, (cj + 1) * L)
+            nc.vector.tensor_scalar(out=incr_t[:, c], in0=at_sb[:, c], scalar1=th_hi[:, cj : cj + 1], scalar2=None, op0=ALU.is_gt)
+        w2_diag = w2_t[:].rearrange("q (c w) -> q c w", w=640)[:, :, 0:P]
+        nc.vector.tensor_tensor(out=w2_diag, in0=w2_diag, in1=ioff_b, op=ALU.mult)
+        transpose_back(w2_t, 1)
+        transpose_p(2)
+        nc.vector.tensor_tensor(out=w1_t[:, 0 : 4 * L], in0=incr_t[:], in1=at_sb[:], op=ALU.mult)
+        make_e(1)
+        w1_diag = w1_t[:].rearrange("q (c w) -> q c w", w=640)[:, :, 0:P]
+        nc.vector.tensor_tensor(out=w1_diag, in0=w1_diag, in1=ioff_b, op=ALU.mult)
+        transpose_back(w1_t, 0)
+        transpose_p(3)
+
+        make_ep(1)
+        nc.vector.tensor_tensor(out=w_bf[2][:], in0=am1_g[:], in1=w_bf[1][:], op=ALU.mult)
+        quantise_e(1)
+        quantise_w(1)
+        quantise_ep(1)
+        quantise_w(0)
+        make_e(2)
+        quantise_w(2)
+        make_ep(2)
+        make_e(3)
+        quantise_e(2)
+        make_ep(3)
+        quantise_ep(2)
+        quantise_e(3)
+
+        sgn = keep.tile([P, NT * L], BF16, name="sgn")
+        ssum = keep.tile([P, NT], F32, name="ssum")
         den = keep.tile([P, 2 * NT], F32, name="den")
         rec = keep.tile([P, 2 * NT], F32, name="rec")
         dif = keep.tile([P, NT], F32, name="dif")
         hd = keep.tile([P, NT], F32, name="hd")
         fm = keep.tile([P, NT], F32, name="fm")
-        nc.vector.tensor_scalar(out=den[:, 0:NT], in0=ssum[:], scalar1=0.5, scalar2=0.5 * L + 1.0, op0=ALU.mult, op1=ALU.add)
-        nc.vector.quantize_mx(out=ep_c[:, prev[0]].bitcast(FP8X4), scales=ep_s[:, prev[0]], in_=prev[1][:])
-        nc.vector.tensor_scalar(out=den[:, NT : 2 * NT], in0=den[:, 0:NT], scalar1=-1.0, scalar2=1.0, op0=ALU.add, op1=ALU.max)
-        nc.vector.reciprocal(out=rec[:], in_=den[:])
-        nc.vector.tensor_tensor(out=dif[:], in0=rec[:, NT : 2 * NT], in1=rec[:, 0:NT], op=ALU.subtract)
-        nc.vector.tensor_scalar(out=hd[:], in0=dif[:], scalar1=0.5, scalar2=None, op0=ALU.mult)
-        nc.vector.scalar_tensor_tensor(out=fm[:], in0=dif[:], scalar=0.5, in1=rec[:, 0:NT], op0=ALU.mult, op1=ALU.add)
 
-        NP = NT // 2
+        def sign_pass(r):
+            nc.scalar.activation(
+                out=sgn[:, r * L : (r + 1) * L],
+                in_=p_sb[:, r * L : (r + 1) * L],
+                func=ACT.Sign,
+                bias=-0.6,
+                scale=1.0,
+                accum_out=ssum[:, r : r + 1],
+            )
+
+        def row_factors(b, between):
+            cs = slice(b * HB, (b + 1) * HB)
+            d0 = slice(2 * b * HB, (2 * b + 1) * HB)
+            d1 = slice((2 * b + 1) * HB, (2 * b + 2) * HB)
+            nc.vector.tensor_scalar(out=den[:, d0], in0=ssum[:, cs], scalar1=0.5, scalar2=0.5 * L + 1.0, op0=ALU.mult, op1=ALU.add)
+            between()
+            nc.vector.tensor_scalar(out=den[:, d1], in0=den[:, d0], scalar1=-1.0, scalar2=1.0, op0=ALU.add, op1=ALU.max)
+            nc.vector.reciprocal(out=rec[:, 2 * b * HB : (2 * b + 2) * HB], in_=den[:, 2 * b * HB : (2 * b + 2) * HB])
+            nc.vector.tensor_tensor(out=dif[:, cs], in0=rec[:, d1], in1=rec[:, d0], op=ALU.subtract)
+            nc.vector.tensor_scalar(out=hd[:, cs], in0=dif[:, cs], scalar1=0.5, scalar2=None, op0=ALU.mult)
+            nc.vector.scalar_tensor_tensor(out=fm[:, cs], in0=dif[:, cs], scalar=0.5, in1=rec[:, d0], op0=ALU.mult, op1=ALU.add)
+
         f_ts = [None] * NP
         u_ts = [None] * NP
 
+        def factor_pass(r2):
+            f_ts[r2] = work.tile([P, 2 * L], F32, name="f_t", bufs=NP)
+            for k in range(2):
+                r = r2 * 2 + k
+                nc.scalar.activation(
+                    out=f_ts[r2][:, k * L : (k + 1) * L],
+                    in_=sgn[:, r * L : (r + 1) * L],
+                    func=ACT.Identity,
+                    bias=fm[:, r : r + 1],
+                    scale=hd[:, r : r + 1],
+                )
+
         def products_and_add(r2):
-            f_t = work.tile([P, 2 * L], F32, name="f_t", bufs=NP)
-            u_t = work.tile([P, 2 * L], F32, name="u_t")
-            f_ts[r2] = f_t
-            u_ts[r2] = u_t
+            u_ts[r2] = work.tile([P, 2 * L], F32, name="u_t")
             for k in range(2):
                 r = r2 * 2 + k
                 mcols = slice(r * P, (r + 1) * P)
-                acc = ps_a.tile([P, L], F32, name="acc")
+                acc = ps_a.tile([P, L], F32, name="acc", tag="acc")
                 ops = [(ep_c, ep_s, 0), (e_c, e_s, 1), (ep_c, ep_s, 2)]
                 for n, (c, s, i) in enumerate(ops):
                     nc.tensor.matmul_mx(
@@ -169,14 +271,7 @@ def tile_labelsmoothloss_pa_kernel(tc, predicts, adjList, label_prob_vec, out):
                         start=(n == 0),
                         stop=(n == 2),
                     )
-                nc.scalar.activation(
-                    out=f_t[:, k * L : (k + 1) * L],
-                    in_=sgn[:, r * L : (r + 1) * L],
-                    func=ACT.Identity,
-                    bias=fm[:, r : r + 1],
-                    scale=hd[:, r : r + 1],
-                )
-                nc.vector.tensor_tensor(out=u_t[:, k * L : (k + 1) * L], in0=acc[:], in1=p_sb[:, r * L : (r + 1) * L], op=ALU.add)
+                nc.vector.tensor_tensor(out=u_ts[r2][:, k * L : (k + 1) * L], in0=acc[:], in1=p_sb[:, r * L : (r + 1) * L], op=ALU.add)
 
         def scale_and_store(r2, pieces):
             o_t = work.tile([P, 2 * L], F32, name="o_t")
@@ -186,8 +281,29 @@ def tile_labelsmoothloss_pa_kernel(tc, predicts, adjList, label_prob_vec, out):
                 nc.vector.tensor_tensor(out=o_t[:, c], in0=u_ts[r2][:, c], in1=f_ts[r2][:, c], op=ALU.mult)
                 nc.sync.dma_start(out=out_dram[:, r2 * 2 * L + k * w : r2 * 2 * L + (k + 1) * w], in_=o_t[:, c])
 
+        for r in range(HB):
+            sign_pass(r)
+        row_factors(0, lambda: quantise_ep(3))
+        factor_pass(0)
+        factor_pass(1)
+        for r in range(HB, HB + 4):
+            sign_pass(r)
+        factor_pass(2)
+        for r in range(HB + 4, NT):
+            sign_pass(r)
+        factor_pass(3)
+
         products_and_add(0)
-        for r2 in range(1, NP):
+        products_and_add(1)
+        scale_and_store(0, 1)
+        products_and_add(2)
+        scale_and_store(1, 1)
+        products_and_add(3)
+        scale_and_store(2, 1)
+        row_factors(1, lambda: None)
+        for r2 in range(4, NP):
+            factor_pass(r2)
+        for r2 in range(4, NP):
             products_and_add(r2)
             scale_and_store(r2 - 1, 1)
         scale_and_store(NP - 1, 2)

@@ -213,7 +213,6 @@ def tile_labelsmoothloss_pa_kernel(tc, predicts, adjList, label_prob_vec, out):
         ssum = keep.tile([P, NT], F32, name="ssum")
         den = keep.tile([P, 2 * NT], F32, name="den")
         rec = keep.tile([P, 2 * NT], F32, name="rec")
-        dif = keep.tile([P, NT], F32, name="dif")
         hd = keep.tile([P, NT], F32, name="hd")
         fm = keep.tile([P, NT], F32, name="fm")
 
@@ -227,83 +226,83 @@ def tile_labelsmoothloss_pa_kernel(tc, predicts, adjList, label_prob_vec, out):
                 accum_out=ssum[:, r : r + 1],
             )
 
-        def row_factors(b, between):
+        def row_factors(b):
             cs = slice(b * HB, (b + 1) * HB)
             d0 = slice(2 * b * HB, (2 * b + 1) * HB)
             d1 = slice((2 * b + 1) * HB, (2 * b + 2) * HB)
-            nc.vector.tensor_scalar(out=den[:, d0], in0=ssum[:, cs], scalar1=0.5, scalar2=0.5 * L + 1.0, op0=ALU.mult, op1=ALU.add)
-            between()
-            nc.vector.tensor_scalar(out=den[:, d1], in0=den[:, d0], scalar1=-1.0, scalar2=1.0, op0=ALU.add, op1=ALU.max)
+            nc.vector.tensor_scalar(out=den[:, d0], in0=ssum[:, cs], scalar1=float(L + 2), scalar2=None, op0=ALU.add)
+            nc.vector.tensor_scalar(out=den[:, d1], in0=ssum[:, cs], scalar1=float(L), scalar2=2.0, op0=ALU.add, op1=ALU.max)
             nc.vector.reciprocal(out=rec[:, 2 * b * HB : (2 * b + 2) * HB], in_=den[:, 2 * b * HB : (2 * b + 2) * HB])
-            nc.vector.tensor_tensor(out=dif[:, cs], in0=rec[:, d1], in1=rec[:, d0], op=ALU.subtract)
-            nc.vector.tensor_scalar(out=hd[:, cs], in0=dif[:, cs], scalar1=0.5, scalar2=None, op0=ALU.mult)
-            nc.vector.scalar_tensor_tensor(out=fm[:, cs], in0=dif[:, cs], scalar=0.5, in1=rec[:, d0], op0=ALU.mult, op1=ALU.add)
+            nc.vector.tensor_tensor(out=hd[:, cs], in0=rec[:, d1], in1=rec[:, d0], op=ALU.subtract)
+            nc.vector.tensor_tensor(out=fm[:, cs], in0=rec[:, d1], in1=rec[:, d0], op=ALU.add)
 
-        f_ts = [None] * NP
-        u_ts = [None] * NP
+        f_all = keep.tile([P, NT * L], F32, name="f_all")
+        TRI = 3
+        u_ts = [None] * (NT // TRI + 1)
+        o_ts = [None] * (NT // TRI + 1)
 
-        def factor_pass(r2):
-            f_ts[r2] = work.tile([P, 2 * L], F32, name="f_t", bufs=NP)
-            for k in range(2):
-                r = r2 * 2 + k
-                nc.scalar.activation(
-                    out=f_ts[r2][:, k * L : (k + 1) * L],
-                    in_=sgn[:, r * L : (r + 1) * L],
-                    func=ACT.Identity,
-                    bias=fm[:, r : r + 1],
-                    scale=hd[:, r : r + 1],
+        def factor_pass(r):
+            nc.scalar.activation(
+                out=f_all[:, r * L : (r + 1) * L],
+                in_=sgn[:, r * L : (r + 1) * L],
+                func=ACT.Identity,
+                bias=fm[:, r : r + 1],
+                scale=hd[:, r : r + 1],
+            )
+
+        def products_and_add(r):
+            k = r % TRI
+            if u_ts[r // TRI] is None:
+                u_ts[r // TRI] = work.tile([P, TRI * L], F32, name="u_t")
+            mcols = slice(r * P, (r + 1) * P)
+            acc = ps_a.tile([P, L], F32, name="acc", tag="acc")
+            ops = [(ep_c, ep_s, 0), (e_c, e_s, 1), (ep_c, ep_s, 2)]
+            for n, (c, s, i) in enumerate(ops):
+                nc.tensor.matmul_mx(
+                    out=acc[:],
+                    lhsT=c[:, mcols].bitcast(FP8X4),
+                    lhsT_scale=s[:, mcols],
+                    rhs=w_c[i][:].bitcast(FP8X4),
+                    rhs_scale=w_s[i][:],
+                    start=(n == 0),
+                    stop=(n == 2),
                 )
+            nc.vector.tensor_tensor(out=u_ts[r // TRI][:, k * L : (k + 1) * L], in0=acc[:], in1=p_sb[:, r * L : (r + 1) * L], op=ALU.add)
 
-        def products_and_add(r2):
-            u_ts[r2] = work.tile([P, 2 * L], F32, name="u_t")
-            for k in range(2):
-                r = r2 * 2 + k
-                mcols = slice(r * P, (r + 1) * P)
-                acc = ps_a.tile([P, L], F32, name="acc", tag="acc")
-                ops = [(ep_c, ep_s, 0), (e_c, e_s, 1), (ep_c, ep_s, 2)]
-                for n, (c, s, i) in enumerate(ops):
-                    nc.tensor.matmul_mx(
-                        out=acc[:],
-                        lhsT=c[:, mcols].bitcast(FP8X4),
-                        lhsT_scale=s[:, mcols],
-                        rhs=w_c[i][:].bitcast(FP8X4),
-                        rhs_scale=w_s[i][:],
-                        start=(n == 0),
-                        stop=(n == 2),
-                    )
-                nc.vector.tensor_tensor(out=u_ts[r2][:, k * L : (k + 1) * L], in0=acc[:], in1=p_sb[:, r * L : (r + 1) * L], op=ALU.add)
+        def scale_and_store(eng, c0, width):
+            t = c0 // (TRI * L)
+            if o_ts[t] is None:
+                o_ts[t] = work.tile([P, TRI * L], F32, name="o_t")
+            c = slice(c0 - t * TRI * L, c0 - t * TRI * L + width)
+            eng.tensor_tensor(out=o_ts[t][:, c], in0=u_ts[t][:, c], in1=f_all[:, c0 : c0 + width], op=ALU.mult)
+            nc.sync.dma_start(out=out_dram[:, c0 : c0 + width], in_=o_ts[t][:, c])
 
-        def scale_and_store(r2, pieces):
-            o_t = work.tile([P, 2 * L], F32, name="o_t")
-            w = 2 * L // pieces
-            for k in range(pieces):
-                c = slice(k * w, (k + 1) * w)
-                nc.vector.tensor_tensor(out=o_t[:, c], in0=u_ts[r2][:, c], in1=f_ts[r2][:, c], op=ALU.mult)
-                nc.sync.dma_start(out=out_dram[:, r2 * 2 * L + k * w : r2 * 2 * L + (k + 1) * w], in_=o_t[:, c])
-
-        for r in range(HB):
+        for r in range(12):
             sign_pass(r)
-        row_factors(0, lambda: quantise_ep(3))
-        factor_pass(0)
-        factor_pass(1)
-        for r in range(HB, HB + 4):
+        row_factors(0)
+        quantise_ep(3)
+        for r in range(5):
+            factor_pass(r)
+        for r in range(12, NT):
             sign_pass(r)
-        factor_pass(2)
-        for r in range(HB + 4, NT):
-            sign_pass(r)
-        factor_pass(3)
+        for r in range(5, HB):
+            factor_pass(r)
 
         products_and_add(0)
         products_and_add(1)
-        scale_and_store(0, 1)
-        products_and_add(2)
-        scale_and_store(1, 1)
-        products_and_add(3)
-        scale_and_store(2, 1)
-        row_factors(1, lambda: None)
-        for r2 in range(4, NP):
-            factor_pass(r2)
-        for r2 in range(4, NP):
-            products_and_add(r2)
-            scale_and_store(r2 - 1, 1)
-        scale_and_store(NP - 1, 2)
+        for t in range(4):
+            products_and_add(TRI * t + 2)
+            scale_and_store(nc.gpsimd, (TRI * t + 2) * L, L)
+            products_and_add(TRI * t + 3)
+            products_and_add(TRI * t + 4)
+            scale_and_store(nc.vector, TRI * t * L, 2 * L)
+            if t == 1:
+                row_factors(1)
+                for r in range(HB, NT):
+                    factor_pass(r)
+        products_and_add(14)
+        products_and_add(15)
+        scale_and_store(nc.vector, 12 * L, 2 * L)
+        scale_and_store(nc.vector, 14 * L, L)
+        scale_and_store(nc.vector, 15 * L, L // 2)
+        scale_and_store(nc.vector, 15 * L + L // 2, L // 2)

@@ -237,7 +237,7 @@ def tile_labelsmoothloss_pa_kernel(tc, predicts, adjList, label_prob_vec, out):
             nc.vector.tensor_tensor(out=fm[:, cs], in0=rec[:, d1], in1=rec[:, d0], op=ALU.add)
 
         f_all = keep.tile([P, NT * L], F32, name="f_all")
-        TRI = 3
+        TRI = 4
         u_ts = [None] * (NT // TRI + 1)
         o_ts = [None] * (NT // TRI + 1)
 
@@ -288,21 +288,22 @@ def tile_labelsmoothloss_pa_kernel(tc, predicts, adjList, label_prob_vec, out):
         for r in range(5, HB):
             factor_pass(r)
 
-        products_and_add(0)
-        products_and_add(1)
-        for t in range(4):
-            products_and_add(TRI * t + 2)
-            scale_and_store(nc.gpsimd, (TRI * t + 2) * L, L)
-            products_and_add(TRI * t + 3)
-            products_and_add(TRI * t + 4)
-            scale_and_store(nc.vector, TRI * t * L, 2 * L)
-            if t == 1:
-                row_factors(1)
-                for r in range(HB, NT):
-                    factor_pass(r)
-        products_and_add(14)
-        products_and_add(15)
-        scale_and_store(nc.vector, 12 * L, 2 * L)
-        scale_and_store(nc.vector, 14 * L, L)
+        def run_of_adds(t):
+            products_and_add(TRI * t)
+            scale_and_store(nc.gpsimd, TRI * t * L, L)
+            for k in range(1, TRI):
+                products_and_add(TRI * t + k)
+
+        run_of_adds(0)
+        run_of_adds(1)
+        scale_and_store(nc.vector, L, 3 * L)
+        row_factors(1)
+        for r in range(HB, NT):
+            factor_pass(r)
+        run_of_adds(2)
+        scale_and_store(nc.vector, 5 * L, 3 * L)
+        run_of_adds(3)
+        scale_and_store(nc.vector, 9 * L, 3 * L)
+        scale_and_store(nc.vector, 13 * L, 2 * L)
         scale_and_store(nc.vector, 15 * L, L // 2)
         scale_and_store(nc.vector, 15 * L + L // 2, L // 2)

@@ -43,7 +43,8 @@ def tile_labelsmoothloss_pa_kernel(tc, predicts, adjList, label_prob_vec, out):
             cols = slice(first * L, (first + tiles) * L)
             nc.sync.dma_start(out=p_sb[:, cols], in_=p_dram[:, cols])
 
-        load_p(0, 2)
+        load_p(0, 1)
+        load_p(1, 1)
         load_p(2, 2)
         a_n = keep.tile([P, 4 * L], BF16, name="a_n")
         nc.sync.dma_start(
@@ -73,10 +74,11 @@ def tile_labelsmoothloss_pa_kernel(tc, predicts, adjList, label_prob_vec, out):
             pt_g = grp.tile([P, GT * L], BF16, name="pt_g", bufs=NG, align_bytes=64)
             pt_gs[g] = pt_g
             pt_gw = pt_g[:].bitcast(F32)
-            for h in range(GT // 2):
+            chunks = [(0, 1), (1, 1), (2, 2)] if g == 0 else [(0, 2), (2, 2)]
+            for first, n in chunks:
                 bank = ps_t.tile([P, 512], F32, name="bank")
-                for k in range(4):
-                    r = g * GT + h * 2 + k // 2
+                for k in range(2 * n):
+                    r = g * GT + first + k // 2
                     u = k % 2
                     nc.tensor.transpose(
                         bank[:, k * P : (k + 1) * P],
@@ -84,8 +86,8 @@ def tile_labelsmoothloss_pa_kernel(tc, predicts, adjList, label_prob_vec, out):
                         ident[:],
                     )
                 nc.scalar.copy(
-                    out=pt_gw[:, h * 512 : (h + 1) * 512].rearrange("q (r x u) -> q r x u", r=2, u=2),
-                    in_=bank[:].rearrange("q (r u x) -> q r x u", r=2, u=2),
+                    out=pt_gw[:, first * 256 : (first + n) * 256].rearrange("q (r x u) -> q r x u", r=n, u=2),
+                    in_=bank[:, 0 : n * 256].rearrange("q (r u x) -> q r x u", r=n, u=2),
                 )
 
         e_c = keep.tile([P, NT * P], U32, name="e_c", align_bytes=64)
@@ -163,9 +165,9 @@ def tile_labelsmoothloss_pa_kernel(tc, predicts, adjList, label_prob_vec, out):
             scale=1.0,
         )
 
-        for h in range(2):
-            make_e(0, slice(h * 2 * L, (h + 1) * 2 * L))
-            make_ep(0, slice(h * 2 * L, (h + 1) * 2 * L))
+        for c in (slice(0, L), slice(L, 2 * L), slice(2 * L, 4 * L)):
+            make_e(0, c)
+            make_ep(0, c)
         th_hi = keep.tile([P, 4], F32, name="th_hi")
         th_lo = keep.tile([P, 4], F32, name="th_lo")
         nc.vector.tensor_scalar(out=th_hi[:], in0=lp_t[:, 0:4], scalar1=0.05, scalar2=None, op0=ALU.add)
@@ -237,9 +239,8 @@ def tile_labelsmoothloss_pa_kernel(tc, predicts, adjList, label_prob_vec, out):
             nc.vector.tensor_tensor(out=fm[:, cs], in0=rec[:, d1], in1=rec[:, d0], op=ALU.add)
 
         f_all = keep.tile([P, NT * L], F32, name="f_all")
-        TRI = 4
-        u_ts = [None] * (NT // TRI + 1)
-        o_ts = [None] * (NT // TRI + 1)
+        RUN = 8
+        u_ts = [None] * (NT // RUN)
 
         def factor_pass(r):
             nc.scalar.activation(
@@ -251,9 +252,9 @@ def tile_labelsmoothloss_pa_kernel(tc, predicts, adjList, label_prob_vec, out):
             )
 
         def products_and_add(r):
-            k = r % TRI
-            if u_ts[r // TRI] is None:
-                u_ts[r // TRI] = work.tile([P, TRI * L], F32, name="u_t")
+            k = r % RUN
+            if u_ts[r // RUN] is None:
+                u_ts[r // RUN] = work.tile([P, RUN * L], F32, name="u_t", bufs=2)
             mcols = slice(r * P, (r + 1) * P)
             acc = ps_a.tile([P, L], F32, name="acc", tag="acc")
             ops = [(ep_c, ep_s, 0), (e_c, e_s, 1), (ep_c, ep_s, 2)]
@@ -267,43 +268,42 @@ def tile_labelsmoothloss_pa_kernel(tc, predicts, adjList, label_prob_vec, out):
                     start=(n == 0),
                     stop=(n == 2),
                 )
-            nc.vector.tensor_tensor(out=u_ts[r // TRI][:, k * L : (k + 1) * L], in0=acc[:], in1=p_sb[:, r * L : (r + 1) * L], op=ALU.add)
+            nc.vector.tensor_tensor(out=u_ts[r // RUN][:, k * L : (k + 1) * L], in0=acc[:], in1=p_sb[:, r * L : (r + 1) * L], op=ALU.add)
 
         def scale_and_store(eng, c0, width):
-            t = c0 // (TRI * L)
-            if o_ts[t] is None:
-                o_ts[t] = work.tile([P, TRI * L], F32, name="o_t")
-            c = slice(c0 - t * TRI * L, c0 - t * TRI * L + width)
-            eng.tensor_tensor(out=o_ts[t][:, c], in0=u_ts[t][:, c], in1=f_all[:, c0 : c0 + width], op=ALU.mult)
-            nc.sync.dma_start(out=out_dram[:, c0 : c0 + width], in_=o_ts[t][:, c])
+            t = c0 // (RUN * L)
+            c = slice(c0 - t * RUN * L, c0 - t * RUN * L + width)
+            o_t = work.tile([P, 2 * L], F32, name="o_t", bufs=4)
+            eng.tensor_tensor(out=o_t[:, 0:width], in0=u_ts[t][:, c], in1=f_all[:, c0 : c0 + width], op=ALU.mult)
+            nc.sync.dma_start(out=out_dram[:, c0 : c0 + width], in_=o_t[:, 0:width])
+
+        GP = 3
+
+        def run_of_adds(t):
+            for k in range(RUN):
+                products_and_add(RUN * t + k)
+                if k < GP:
+                    scale_and_store(nc.gpsimd, (RUN * t + k) * L, L)
 
         for r in range(12):
             sign_pass(r)
         row_factors(0)
         quantise_ep(3)
-        for r in range(5):
+        for r in range(GP):
             factor_pass(r)
         for r in range(12, NT):
             sign_pass(r)
-        for r in range(5, HB):
+        for r in range(GP, HB):
             factor_pass(r)
 
-        def run_of_adds(t):
-            products_and_add(TRI * t)
-            scale_and_store(nc.gpsimd, TRI * t * L, L)
-            for k in range(1, TRI):
-                products_and_add(TRI * t + k)
-
         run_of_adds(0)
-        run_of_adds(1)
-        scale_and_store(nc.vector, L, 3 * L)
         row_factors(1)
         for r in range(HB, NT):
             factor_pass(r)
-        run_of_adds(2)
-        scale_and_store(nc.vector, 5 * L, 3 * L)
-        run_of_adds(3)
-        scale_and_store(nc.vector, 9 * L, 3 * L)
+        for r in range(GP, RUN):
+            scale_and_store(nc.vector, r * L, L)
+        run_of_adds(1)
+        scale_and_store(nc.vector, 11 * L, 2 * L)
         scale_and_store(nc.vector, 13 * L, 2 * L)
         scale_and_store(nc.vector, 15 * L, L // 2)
         scale_and_store(nc.vector, 15 * L + L // 2, L // 2)

@@ -14,11 +14,17 @@ ACT = mybir.ActivationFunctionType
 P = 128
 B = 2048
 L = 512
+PACK = 4
+LW = L // 2
 NT = B // P
-GT = 4
-NG = NT // GT
-NP = NT // 2
-HB = NT // 2
+NC = L // P
+PREDICT_LIMIT = 0.6
+RELATION_GAP = 0.05
+DIAG_STEP = L + P
+RUN = 8
+ON_GPSIMD = 3
+EARLY_SIGNS = 12
+STAT = NT // 2
 FLOPS = 3 * 2 * B * L * L
 
 
@@ -26,284 +32,295 @@ def tile_labelsmoothloss_pa_kernel(tc, predicts, adjList, label_prob_vec, out):
     nc = tc.nc
     with ExitStack() as ctx:
         keep = ctx.enter_context(tc.tile_pool(name="keep", bufs=1))
-        grp = ctx.enter_context(tc.tile_pool(name="grp", bufs=2))
-        work = ctx.enter_context(tc.tile_pool(name="work", bufs=3))
+        ring = ctx.enter_context(tc.tile_pool(name="ring", bufs=2))
         ps_t = ctx.enter_context(tc.psum_pool(name="ps_t", bufs=2))
         ps_a = ctx.enter_context(tc.psum_pool(name="ps_a", bufs=6))
         ctx.enter_context(tc.manual_schedule())
 
-        lp_rows = keep.tile([P, P], BF16, name="lp_rows")
-        nc.vector.memset(lp_rows[:], 0.0)
-        nc.scalar.dma_start(out=lp_rows[0:4, :], in_=label_prob_vec.rearrange("(c p) -> c p", p=P))
-        p_sb = keep.tile([P, NT * L], BF16, name="p_sb")
         p_dram = predicts.rearrange("(x r) j -> x (r j)", r=NT)
         out_dram = out.rearrange("(x r) j -> x (r j)", r=NT)
+
+        lp_rows = keep.tile([P, P], BF16, name="lp_rows")
+        nc.vector.memset(lp_rows[:], 0.0)
+        nc.scalar.dma_start(out=lp_rows[0:NC, :], in_=label_prob_vec.rearrange("(c p) -> c p", p=P))
+
+        p_sb = keep.tile([P, NT * L], BF16, name="p_sb")
 
         def load_p(first, tiles):
             cols = slice(first * L, (first + tiles) * L)
             nc.sync.dma_start(out=p_sb[:, cols], in_=p_dram[:, cols])
 
+        a_rows = keep.tile([P, NC * L], BF16, name="a_rows")
+        a_words = keep.tile([P, PACK * L], BF16, name="a_words")
         load_p(0, 1)
         load_p(1, 1)
         load_p(2, 2)
-        a_n = keep.tile([P, 4 * L], BF16, name="a_n")
         nc.sync.dma_start(
-            out=a_n[:].rearrange("p (c j) -> p c j", c=4),
+            out=a_rows[:].rearrange("p (c j) -> p c j", c=NC),
             in_=adjList.rearrange("(c p) j -> p c j", p=P),
         )
-        load_p(GT, GT)
-        a_q = keep.tile([P, 4 * L], BF16, name="a_q")
+        load_p(4, 4)
         nc.sync.dma_start(
-            out=a_q[:].rearrange("q (u w) -> q u w", u=2),
+            out=a_words[:].rearrange("q (u w) -> q u w", u=2),
             in_=adjList.rearrange("(u q e) j -> q u (e j)", u=2, e=2),
         )
-        for g in range(2, NG):
-            load_p(g * GT, GT)
+        load_p(8, 4)
+        load_p(12, 4)
 
         ident = keep.tile([P, P], F32, name="ident")
         make_identity(nc, ident[:])
         ident_b = keep.tile([P, P], BF16, name="ident_b")
         make_identity(nc, ident_b[:])
-        ioff = keep.tile([P, P], BF16, name="ioff")
-        nc.vector.tensor_scalar(out=ioff[:], in0=ident[:], scalar1=-1.0, scalar2=1.0, op0=ALU.mult, op1=ALU.add)
+        off_diag = keep.tile([P, P], BF16, name="off_diag")
+        nc.vector.tensor_scalar(out=off_diag[:], in0=ident[:], scalar1=-1.0, scalar2=1.0, op0=ALU.mult, op1=ALU.add)
 
         p_words = p_sb[:].bitcast(F32)
-        pt_gs = [None] * NG
+        p_t = keep.tile([P, NT * L], BF16, name="p_t", align_bytes=64)
+        p_t_words = p_t[:].bitcast(F32)
+        e_codes = keep.tile([P, NT * P], U32, name="e_codes", align_bytes=64)
+        e_scales = keep.tile([P, NT * P], U8, name="e_scales", align_bytes=64)
+        ep_codes = keep.tile([P, NT * P], U32, name="ep_codes", align_bytes=64)
+        ep_scales = keep.tile([P, NT * P], U8, name="ep_scales", align_bytes=64)
 
-        def transpose_p(g):
-            pt_g = grp.tile([P, GT * L], BF16, name="pt_g", bufs=NG, align_bytes=64)
-            pt_gs[g] = pt_g
-            pt_gw = pt_g[:].bitcast(F32)
-            chunks = [(0, 1), (1, 1), (2, 2)] if g == 0 else [(0, 2), (2, 2)]
-            for first, n in chunks:
-                bank = ps_t.tile([P, 512], F32, name="bank")
-                for k in range(2 * n):
-                    r = g * GT + first + k // 2
-                    u = k % 2
-                    nc.tensor.transpose(
-                        bank[:, k * P : (k + 1) * P],
-                        p_words[:, r * 256 + u * P : r * 256 + (u + 1) * P],
-                        ident[:],
-                    )
-                nc.scalar.copy(
-                    out=pt_gw[:, first * 256 : (first + n) * 256].rearrange("q (r x u) -> q r x u", r=n, u=2),
-                    in_=bank[:, 0 : n * 256].rearrange("q (r u x) -> q r x u", r=n, u=2),
-                )
+        def transpose_p(first, tiles):
+            bank = ps_t.tile([P, 2 * LW], F32, name="bank")
+            for k in range(2 * tiles):
+                w0 = (first + k // 2) * LW + (k % 2) * P
+                nc.tensor.transpose(bank[:, k * P : (k + 1) * P], p_words[:, w0 : w0 + P], ident[:])
+            nc.scalar.copy(
+                out=p_t_words[:, first * LW : (first + tiles) * LW].rearrange("q (r x u) -> q r x u", r=tiles, u=2),
+                in_=bank[:, 0 : tiles * LW].rearrange("q (r u x) -> q r x u", r=tiles, u=2),
+            )
 
-        e_c = keep.tile([P, NT * P], U32, name="e_c", align_bytes=64)
-        e_s = keep.tile([P, NT * P], U8, name="e_s", align_bytes=64)
-        ep_c = keep.tile([P, NT * P], U32, name="ep_c", align_bytes=64)
-        ep_s = keep.tile([P, NT * P], U8, name="ep_s", align_bytes=64)
-        et_gs = [None] * NG
-        ept_gs = [None] * NG
+        mask_tiles = {}
 
-        WHOLE = slice(0, GT * L)
+        def new_masks(first, tiles):
+            e_t = ring.tile([P, RUN * L], BF16, name="e_t", align_bytes=64)
+            ep_t = ring.tile([P, RUN * L], BF16, name="ep_t", align_bytes=64)
+            mask_tiles[first] = (e_t, ep_t, tiles)
 
-        def make_e(g, c=WHOLE):
-            if et_gs[g] is None:
-                et_gs[g] = grp.tile([P, GT * L], BF16, name="et_g", align_bytes=64)
-            nc.vector.tensor_scalar(out=et_gs[g][:, c], in0=pt_gs[g][:, c], scalar1=0.6, scalar2=None, op0=ALU.is_gt)
+        def make_e(group, first, tiles):
+            c = slice((first - group) * L, (first - group + tiles) * L)
+            nc.vector.tensor_scalar(
+                out=mask_tiles[group][0][:, c],
+                in0=p_t[:, first * L : (first + tiles) * L],
+                scalar1=PREDICT_LIMIT,
+                scalar2=None,
+                op0=ALU.is_gt,
+            )
 
-        def make_ep(g, c=WHOLE):
-            if ept_gs[g] is None:
-                ept_gs[g] = grp.tile([P, GT * L], BF16, name="ept_g", align_bytes=64)
-            nc.vector.tensor_tensor(out=ept_gs[g][:, c], in0=et_gs[g][:, c], in1=pt_gs[g][:, c], op=ALU.mult)
+        def make_ep(group, first, tiles):
+            c = slice((first - group) * L, (first - group + tiles) * L)
+            nc.vector.tensor_tensor(
+                out=mask_tiles[group][1][:, c],
+                in0=mask_tiles[group][0][:, c],
+                in1=p_t[:, first * L : (first + tiles) * L],
+                op=ALU.mult,
+            )
 
-        def quantise_e(g):
-            wcols = slice(g * GT * P, (g + 1) * GT * P)
-            nc.vector.quantize_mx(out=e_c[:, wcols].bitcast(FP8X4), scales=e_s[:, wcols], in_=et_gs[g][:])
+        def quantise_masks(group, which):
+            tiles = mask_tiles[group][2]
+            codes, scales = ((e_codes, e_scales), (ep_codes, ep_scales))[which]
+            words = slice(group * P, (group + tiles) * P)
+            nc.vector.quantize_mx(
+                out=codes[:, words].bitcast(FP8X4),
+                scales=scales[:, words],
+                in_=mask_tiles[group][which][:, 0 : tiles * L],
+            )
 
-        def quantise_ep(g):
-            wcols = slice(g * GT * P, (g + 1) * GT * P)
-            nc.vector.quantize_mx(out=ep_c[:, wcols].bitcast(FP8X4), scales=ep_s[:, wcols], in_=ept_gs[g][:])
+        w_bf = [keep.tile([P, PACK * L], BF16, name="w_bf%d" % n, align_bytes=64) for n in range(3)]
+        w_codes = [keep.tile([P, L], U32, name="w_codes%d" % n, align_bytes=64) for n in range(3)]
+        w_scales = [keep.tile([P, L], U8, name="w_scales%d" % n, align_bytes=64) for n in range(3)]
 
-        w_bf = [keep.tile([P, 4 * L], BF16, name="w_bf%d" % i, align_bytes=64) for i in range(3)]
-        w_c = [keep.tile([P, L], U32, name="w_c%d" % i, align_bytes=64) for i in range(3)]
-        w_s = [keep.tile([P, L], U8, name="w_s%d" % i, align_bytes=64) for i in range(3)]
+        def quantise_w(n):
+            nc.vector.quantize_mx(out=w_codes[n][:].bitcast(FP8X4), scales=w_scales[n][:], in_=w_bf[n][:])
 
-        def quantise_w(i):
-            nc.vector.quantize_mx(out=w_c[i][:].bitcast(FP8X4), scales=w_s[i][:], in_=w_bf[i][:])
+        a_t = keep.tile([P, NC * L], BF16, name="a_t")
+        th_hi = keep.tile([P, NC], F32, name="th_hi")
+        th_lo = keep.tile([P, NC], F32, name="th_lo")
+        incr_t = keep.tile([P, NC * L], BF16, name="incr_t")
+        incr_a_t = keep.tile([P, NC * DIAG_STEP], BF16, name="incr_a_t")
+        decr_t = keep.tile([P, NC * DIAG_STEP], BF16, name="decr_t")
+        a_minus_1 = keep.tile([P, PACK * L], BF16, name="a_minus_1")
 
-        def transpose_back(src, i):
-            src_w = src[:, 0 : 4 * L].bitcast(F32)
-            dst_w = w_bf[i][:].bitcast(F32)
-            for b in range(2):
-                wb = ps_a.tile([P, 512], F32, name="wb", tag="acc")
-                for cc in range(2):
-                    for u in range(2):
+        def transpose_lp():
+            lp_t = ps_a.tile([P, P], BF16, name="lp_t", tag="acc")
+            nc.tensor.transpose(lp_t[:], lp_rows[:], ident_b[:])
+            return lp_t
+
+        def transpose_a():
+            for side in range(2):
+                bank = ps_a.tile([P, 2 * L], BF16, name="a_bank", tag="acc")
+                for k in range(2):
+                    c = 2 * side + k
+                    for ci in range(NC):
                         nc.tensor.transpose(
-                            wb[:, u * 256 + cc * P : u * 256 + (cc + 1) * P],
-                            src_w[:, (2 * b + cc) * 256 + u * P : (2 * b + cc) * 256 + (u + 1) * P],
-                            ident[:],
+                            bank[:, k * L + ci * P : k * L + (ci + 1) * P],
+                            a_rows[:, ci * L + c * P : ci * L + (c + 1) * P],
+                            ident_b[:],
                         )
+                nc.scalar.copy(out=a_t[:, side * 2 * L : (side + 1) * 2 * L], in_=bank[:])
+
+        def compare(dst, threshold, op):
+            for c in range(NC):
+                cols = slice(c * L, (c + 1) * L)
+                nc.vector.tensor_scalar(out=dst[:, cols], in0=a_t[:, cols], scalar1=threshold[:, c : c + 1], scalar2=None, op0=op)
+
+        def clear_diagonal(m_t):
+            blocks = m_t[:].rearrange("q (c w) -> q c w", w=DIAG_STEP)[:, :, 0:P]
+            nc.vector.tensor_tensor(out=blocks, in0=blocks, in1=off_diag[:].unsqueeze(1).to_broadcast([P, NC, P]), op=ALU.mult)
+
+        def transpose_back(m_t, n):
+            src = m_t[:, 0 : NC * L].bitcast(F32)
+            dst = w_bf[n][:].bitcast(F32)
+            for side in range(2):
+                bank = ps_a.tile([P, 2 * LW], F32, name="w_bank", tag="acc")
+                for k in range(2):
+                    for u in range(2):
+                        w0 = (2 * side + k) * LW + u * P
+                        nc.tensor.transpose(bank[:, u * LW + k * P : u * LW + (k + 1) * P], src[:, w0 : w0 + P], ident[:])
                 nc.scalar.copy(
-                    out=dst_w[:, b * 512 : (b + 1) * 512].rearrange("q (j u) -> q j u", u=2),
-                    in_=wb[:].rearrange("q (u j) -> q j u", u=2),
+                    out=dst[:, side * 2 * LW : (side + 1) * 2 * LW].rearrange("q (j u) -> q j u", u=2),
+                    in_=bank[:].rearrange("q (u j) -> q j u", u=2),
                 )
 
-        transpose_p(0)
-        lp_t = ps_a.tile([P, P], BF16, name="lp_t", tag="acc")
-        nc.tensor.transpose(lp_t[:], lp_rows[:], ident_b[:])
-        at_sb = keep.tile([P, 4 * L], BF16, name="at_sb")
-        for b in range(2):
-            at_ps = ps_a.tile([P, 2 * L], BF16, name="at_ps", tag="acc")
-            for cc in range(2):
-                for c in range(4):
-                    nc.tensor.transpose(
-                        at_ps[:, cc * L + c * P : cc * L + (c + 1) * P],
-                        a_n[:, c * L + (2 * b + cc) * P : c * L + (2 * b + cc + 1) * P],
-                        ident_b[:],
-                    )
-            nc.scalar.copy(out=at_sb[:, b * 2 * L : (b + 1) * 2 * L], in_=at_ps[:])
-        transpose_p(1)
-        am1_g = keep.tile([P, 4 * L], BF16, name="am1_g")
+        sgn = keep.tile([P, NT * L], BF16, name="sgn")
+        sgn_sum = keep.tile([P, NT], F32, name="sgn_sum")
+        twice_rel = keep.tile([P, 2 * NT], F32, name="twice_rel")
+        half_r = keep.tile([P, 2 * NT], F32, name="half_r")
+        step = keep.tile([P, NT], F32, name="step")
+        mid = keep.tile([P, NT], F32, name="mid")
+        factor = keep.tile([P, NT * L], F32, name="factor")
+
+        def sign_pass(r):
+            cols = slice(r * L, (r + 1) * L)
+            nc.scalar.activation(
+                out=sgn[:, cols], in_=p_sb[:, cols], func=ACT.Sign, bias=-PREDICT_LIMIT, scale=1.0, accum_out=sgn_sum[:, r : r + 1]
+            )
+
+        def row_factors(batch):
+            rows = slice(batch * STAT, (batch + 1) * STAT)
+            both = slice(2 * batch * STAT, (2 * batch + 2) * STAT)
+            for_0 = slice(2 * batch * STAT, (2 * batch + 1) * STAT)
+            for_1 = slice((2 * batch + 1) * STAT, (2 * batch + 2) * STAT)
+            nc.vector.tensor_scalar(out=twice_rel[:, for_0], in0=sgn_sum[:, rows], scalar1=float(L + 2), scalar2=None, op0=ALU.add)
+            nc.vector.tensor_scalar(
+                out=twice_rel[:, for_1], in0=sgn_sum[:, rows], scalar1=float(L), scalar2=2.0, op0=ALU.add, op1=ALU.max
+            )
+            nc.vector.reciprocal(out=half_r[:, both], in_=twice_rel[:, both])
+            nc.vector.tensor_tensor(out=step[:, rows], in0=half_r[:, for_1], in1=half_r[:, for_0], op=ALU.subtract)
+            nc.vector.tensor_tensor(out=mid[:, rows], in0=half_r[:, for_1], in1=half_r[:, for_0], op=ALU.add)
+
+        def factor_pass(r):
+            cols = slice(r * L, (r + 1) * L)
+            nc.scalar.activation(
+                out=factor[:, cols], in_=sgn[:, cols], func=ACT.Identity, bias=mid[:, r : r + 1], scale=step[:, r : r + 1]
+            )
+
+        num = keep.tile([P, RUN * L], F32, name="num")
+
+        def products_and_add(r):
+            samples = slice(r * P, (r + 1) * P)
+            acc = ps_a.tile([P, L], F32, name="acc", tag="acc")
+            passes = ((ep_codes, ep_scales, 0), (e_codes, e_scales, 1), (ep_codes, ep_scales, 2))
+            for k, (codes, scales, n) in enumerate(passes):
+                nc.tensor.matmul_mx(
+                    out=acc[:],
+                    lhsT=codes[:, samples].bitcast(FP8X4),
+                    lhsT_scale=scales[:, samples],
+                    rhs=w_codes[n][:].bitcast(FP8X4),
+                    rhs_scale=w_scales[n][:],
+                    start=(k == 0),
+                    stop=(k == 2),
+                )
+            nc.vector.tensor_tensor(
+                out=num[:, (r % RUN) * L : (r % RUN + 1) * L], in0=acc[:], in1=p_sb[:, r * L : (r + 1) * L], op=ALU.add
+            )
+
+        def scale_and_store(engine, c0, width):
+            n0 = c0 % (RUN * L)
+            if width > L:
+                res = ring.tile([P, 2 * L], F32, name="res_wide")
+            else:
+                res = ring.tile([P, L], F32, name="res", bufs=8)
+            engine.tensor_tensor(out=res[:, 0:width], in0=num[:, n0 : n0 + width], in1=factor[:, c0 : c0 + width], op=ALU.mult)
+            nc.sync.dma_start(out=out_dram[:, c0 : c0 + width], in_=res[:, 0:width])
+
+        def run_of_adds(first):
+            for r in range(first, first + RUN):
+                products_and_add(r)
+                if r < first + ON_GPSIMD:
+                    scale_and_store(nc.gpsimd, r * L, L)
+
+        transpose_p(0, 1)
+        transpose_p(1, 1)
+        transpose_p(2, 2)
+        lp_t = transpose_lp()
+        transpose_a()
+        transpose_p(4, 2)
+        transpose_p(6, 2)
         nc.scalar.activation(
-            out=am1_g[:].rearrange("q (j t) -> q j t", t=4),
-            in_=a_q[:].rearrange("q (t j) -> q j t", t=4),
+            out=a_minus_1[:].rearrange("q (j t) -> q j t", t=PACK),
+            in_=a_words[:].rearrange("q (t j) -> q j t", t=PACK),
             func=ACT.Identity,
             bias=-1.0,
             scale=1.0,
         )
 
-        for c in (slice(0, L), slice(L, 2 * L), slice(2 * L, 4 * L)):
-            make_e(0, c)
-            make_ep(0, c)
-        th_hi = keep.tile([P, 4], F32, name="th_hi")
-        th_lo = keep.tile([P, 4], F32, name="th_lo")
-        nc.vector.tensor_scalar(out=th_hi[:], in0=lp_t[:, 0:4], scalar1=0.05, scalar2=None, op0=ALU.add)
-        nc.vector.tensor_scalar(out=th_lo[:], in0=lp_t[:, 0:4], scalar1=-0.05, scalar2=None, op0=ALU.add)
-        quantise_e(0)
-        quantise_ep(0)
+        new_masks(0, 4)
+        for first, tiles in ((0, 1), (1, 1), (2, 2)):
+            make_e(0, first, tiles)
+            make_ep(0, first, tiles)
+        nc.vector.tensor_scalar(out=th_hi[:], in0=lp_t[:, 0:NC], scalar1=RELATION_GAP, scalar2=None, op0=ALU.add)
+        nc.vector.tensor_scalar(out=th_lo[:], in0=lp_t[:, 0:NC], scalar1=-RELATION_GAP, scalar2=None, op0=ALU.add)
+        quantise_masks(0, 0)
+        quantise_masks(0, 1)
 
-        incr_t = keep.tile([P, 4 * L], BF16, name="incr_t")
-        w1_t = keep.tile([P, 4 * 640], BF16, name="w1_t")
-        w2_t = keep.tile([P, 4 * 640], BF16, name="w2_t")
-        ioff_b = ioff[:].unsqueeze(1).to_broadcast([P, 4, P])
-        for cj in range(4):
-            c = slice(cj * L, (cj + 1) * L)
-            nc.vector.tensor_scalar(out=w2_t[:, c], in0=at_sb[:, c], scalar1=th_lo[:, cj : cj + 1], scalar2=None, op0=ALU.is_lt)
-        for cj in range(4):
-            c = slice(cj * L, (cj + 1) * L)
-            nc.vector.tensor_scalar(out=incr_t[:, c], in0=at_sb[:, c], scalar1=th_hi[:, cj : cj + 1], scalar2=None, op0=ALU.is_gt)
-        w2_diag = w2_t[:].rearrange("q (c w) -> q c w", w=640)[:, :, 0:P]
-        nc.vector.tensor_tensor(out=w2_diag, in0=w2_diag, in1=ioff_b, op=ALU.mult)
-        transpose_back(w2_t, 1)
-        transpose_p(2)
-        nc.vector.tensor_tensor(out=w1_t[:, 0 : 4 * L], in0=incr_t[:], in1=at_sb[:], op=ALU.mult)
-        make_e(1)
-        w1_diag = w1_t[:].rearrange("q (c w) -> q c w", w=640)[:, :, 0:P]
-        nc.vector.tensor_tensor(out=w1_diag, in0=w1_diag, in1=ioff_b, op=ALU.mult)
-        transpose_back(w1_t, 0)
-        transpose_p(3)
+        compare(decr_t, th_lo, ALU.is_lt)
+        compare(incr_t, th_hi, ALU.is_gt)
+        clear_diagonal(decr_t)
+        transpose_back(decr_t, 1)
+        transpose_p(8, 2)
+        transpose_p(10, 2)
+        nc.vector.tensor_tensor(out=incr_a_t[:, 0 : NC * L], in0=incr_t[:], in1=a_t[:], op=ALU.mult)
+        new_masks(4, 4)
+        make_e(4, 4, 4)
+        clear_diagonal(incr_a_t)
+        transpose_back(incr_a_t, 0)
+        transpose_p(12, 2)
+        transpose_p(14, 2)
 
-        make_ep(1)
-        nc.vector.tensor_tensor(out=w_bf[2][:], in0=am1_g[:], in1=w_bf[1][:], op=ALU.mult)
-        quantise_e(1)
+        make_ep(4, 4, 4)
+        nc.vector.tensor_tensor(out=w_bf[2][:], in0=a_minus_1[:], in1=w_bf[1][:], op=ALU.mult)
+        quantise_masks(4, 0)
         quantise_w(1)
-        quantise_ep(1)
+        quantise_masks(4, 1)
         quantise_w(0)
-        make_e(2)
+        new_masks(8, 8)
+        make_e(8, 8, 8)
         quantise_w(2)
-        make_ep(2)
-        make_e(3)
-        quantise_e(2)
-        make_ep(3)
-        quantise_ep(2)
-        quantise_e(3)
+        make_ep(8, 8, 8)
+        quantise_masks(8, 0)
 
-        sgn = keep.tile([P, NT * L], BF16, name="sgn")
-        ssum = keep.tile([P, NT], F32, name="ssum")
-        den = keep.tile([P, 2 * NT], F32, name="den")
-        rec = keep.tile([P, 2 * NT], F32, name="rec")
-        hd = keep.tile([P, NT], F32, name="hd")
-        fm = keep.tile([P, NT], F32, name="fm")
-
-        def sign_pass(r):
-            nc.scalar.activation(
-                out=sgn[:, r * L : (r + 1) * L],
-                in_=p_sb[:, r * L : (r + 1) * L],
-                func=ACT.Sign,
-                bias=-0.6,
-                scale=1.0,
-                accum_out=ssum[:, r : r + 1],
-            )
-
-        def row_factors(b):
-            cs = slice(b * HB, (b + 1) * HB)
-            d0 = slice(2 * b * HB, (2 * b + 1) * HB)
-            d1 = slice((2 * b + 1) * HB, (2 * b + 2) * HB)
-            nc.vector.tensor_scalar(out=den[:, d0], in0=ssum[:, cs], scalar1=float(L + 2), scalar2=None, op0=ALU.add)
-            nc.vector.tensor_scalar(out=den[:, d1], in0=ssum[:, cs], scalar1=float(L), scalar2=2.0, op0=ALU.add, op1=ALU.max)
-            nc.vector.reciprocal(out=rec[:, 2 * b * HB : (2 * b + 2) * HB], in_=den[:, 2 * b * HB : (2 * b + 2) * HB])
-            nc.vector.tensor_tensor(out=hd[:, cs], in0=rec[:, d1], in1=rec[:, d0], op=ALU.subtract)
-            nc.vector.tensor_tensor(out=fm[:, cs], in0=rec[:, d1], in1=rec[:, d0], op=ALU.add)
-
-        f_all = keep.tile([P, NT * L], F32, name="f_all")
-        RUN = 8
-        u_ts = [None] * (NT // RUN)
-
-        def factor_pass(r):
-            nc.scalar.activation(
-                out=f_all[:, r * L : (r + 1) * L],
-                in_=sgn[:, r * L : (r + 1) * L],
-                func=ACT.Identity,
-                bias=fm[:, r : r + 1],
-                scale=hd[:, r : r + 1],
-            )
-
-        def products_and_add(r):
-            k = r % RUN
-            if u_ts[r // RUN] is None:
-                u_ts[r // RUN] = work.tile([P, RUN * L], F32, name="u_t", bufs=2)
-            mcols = slice(r * P, (r + 1) * P)
-            acc = ps_a.tile([P, L], F32, name="acc", tag="acc")
-            ops = [(ep_c, ep_s, 0), (e_c, e_s, 1), (ep_c, ep_s, 2)]
-            for n, (c, s, i) in enumerate(ops):
-                nc.tensor.matmul_mx(
-                    out=acc[:],
-                    lhsT=c[:, mcols].bitcast(FP8X4),
-                    lhsT_scale=s[:, mcols],
-                    rhs=w_c[i][:].bitcast(FP8X4),
-                    rhs_scale=w_s[i][:],
-                    start=(n == 0),
-                    stop=(n == 2),
-                )
-            nc.vector.tensor_tensor(out=u_ts[r // RUN][:, k * L : (k + 1) * L], in0=acc[:], in1=p_sb[:, r * L : (r + 1) * L], op=ALU.add)
-
-        def scale_and_store(eng, c0, width):
-            t = c0 // (RUN * L)
-            c = slice(c0 - t * RUN * L, c0 - t * RUN * L + width)
-            o_t = work.tile([P, 2 * L], F32, name="o_t", bufs=4)
-            eng.tensor_tensor(out=o_t[:, 0:width], in0=u_ts[t][:, c], in1=f_all[:, c0 : c0 + width], op=ALU.mult)
-            nc.sync.dma_start(out=out_dram[:, c0 : c0 + width], in_=o_t[:, 0:width])
-
-        GP = 3
-
-        def run_of_adds(t):
-            for k in range(RUN):
-                products_and_add(RUN * t + k)
-                if k < GP:
-                    scale_and_store(nc.gpsimd, (RUN * t + k) * L, L)
-
-        for r in range(12):
+        for r in range(EARLY_SIGNS):
             sign_pass(r)
         row_factors(0)
-        quantise_ep(3)
-        for r in range(GP):
+        quantise_masks(8, 1)
+        for r in range(ON_GPSIMD):
             factor_pass(r)
-        for r in range(12, NT):
+        for r in range(EARLY_SIGNS, NT):
             sign_pass(r)
-        for r in range(GP, HB):
+        for r in range(ON_GPSIMD, STAT):
             factor_pass(r)
 
         run_of_adds(0)
         row_factors(1)
-        for r in range(HB, NT):
+        for r in range(STAT, NT):
             factor_pass(r)
-        for r in range(GP, RUN):
+        for r in range(ON_GPSIMD, RUN):
             scale_and_store(nc.vector, r * L, L)
-        run_of_adds(1)
-        scale_and_store(nc.vector, 11 * L, 2 * L)
-        scale_and_store(nc.vector, 13 * L, 2 * L)
-        scale_and_store(nc.vector, 15 * L, L // 2)
-        scale_and_store(nc.vector, 15 * L + L // 2, L // 2)
+        run_of_adds(RUN)
+        scale_and_store(nc.vector, (RUN + ON_GPSIMD) * L, 2 * L)
+        scale_and_store(nc.vector, (RUN + ON_GPSIMD + 2) * L, 2 * L)
+        scale_and_store(nc.vector, (NT - 1) * L, L // 2)
+        scale_and_store(nc.vector, (NT - 1) * L + L // 2, L // 2)

@@ -94,10 +94,10 @@ def tile_labelsmoothloss_pa_kernel(tc, predicts, adjList, label_prob_vec, out):
 
         mask_tiles = {}
 
-        def new_masks(first, tiles):
+        def new_masks(first):
             e_t = ring.tile([P, RUN * L], BF16, name="e_t", align_bytes=64)
             ep_t = ring.tile([P, RUN * L], BF16, name="ep_t", align_bytes=64)
-            mask_tiles[first] = (e_t, ep_t, tiles)
+            mask_tiles[first] = (e_t, ep_t)
 
         def make_e(group, first, tiles):
             c = slice((first - group) * L, (first - group + tiles) * L)
@@ -118,14 +118,13 @@ def tile_labelsmoothloss_pa_kernel(tc, predicts, adjList, label_prob_vec, out):
                 op=ALU.mult,
             )
 
-        def quantise_masks(group, which):
-            tiles = mask_tiles[group][2]
+        def quantise_masks(group, which, first, tiles):
             codes, scales = ((e_codes, e_scales), (ep_codes, ep_scales))[which]
-            words = slice(group * P, (group + tiles) * P)
+            words = slice(first * P, (first + tiles) * P)
             nc.vector.quantize_mx(
                 out=codes[:, words].bitcast(FP8X4),
                 scales=scales[:, words],
-                in_=mask_tiles[group][which][:, 0 : tiles * L],
+                in_=mask_tiles[group][which][:, (first - group) * L : (first - group + tiles) * L],
             )
 
         w_bf = [keep.tile([P, PACK * L], BF16, name="w_bf%d" % n, align_bytes=64) for n in range(3)]
@@ -198,7 +197,7 @@ def tile_labelsmoothloss_pa_kernel(tc, predicts, adjList, label_prob_vec, out):
                 out=sgn[:, cols], in_=p_sb[:, cols], func=ACT.Sign, bias=-PREDICT_LIMIT, scale=1.0, accum_out=sgn_sum[:, r : r + 1]
             )
 
-        def row_factors(batch):
+        def row_factors(batch, filler_1, filler_2):
             rows = slice(batch * STAT, (batch + 1) * STAT)
             both = slice(2 * batch * STAT, (2 * batch + 2) * STAT)
             for_0 = slice(2 * batch * STAT, (2 * batch + 1) * STAT)
@@ -207,7 +206,9 @@ def tile_labelsmoothloss_pa_kernel(tc, predicts, adjList, label_prob_vec, out):
             nc.vector.tensor_scalar(
                 out=twice_rel[:, for_1], in0=sgn_sum[:, rows], scalar1=float(L), scalar2=2.0, op0=ALU.add, op1=ALU.max
             )
+            filler_1()
             nc.vector.reciprocal(out=half_r[:, both], in_=twice_rel[:, both])
+            filler_2()
             nc.vector.tensor_tensor(out=step[:, rows], in0=half_r[:, for_1], in1=half_r[:, for_0], op=ALU.subtract)
             nc.vector.tensor_tensor(out=mid[:, rows], in0=half_r[:, for_1], in1=half_r[:, for_0], op=ALU.add)
 
@@ -267,14 +268,17 @@ def tile_labelsmoothloss_pa_kernel(tc, predicts, adjList, label_prob_vec, out):
             scale=1.0,
         )
 
-        new_masks(0, 4)
-        for first, tiles in ((0, 1), (1, 1), (2, 2)):
-            make_e(0, first, tiles)
-            make_ep(0, first, tiles)
+        new_masks(0)
+        make_e(0, 0, 1)
+        make_e(0, 1, 1)
+        make_ep(0, 0, 1)
+        make_ep(0, 1, 1)
+        make_e(0, 2, 2)
         nc.vector.tensor_scalar(out=th_hi[:], in0=lp_t[:, 0:NC], scalar1=RELATION_GAP, scalar2=None, op0=ALU.add)
         nc.vector.tensor_scalar(out=th_lo[:], in0=lp_t[:, 0:NC], scalar1=-RELATION_GAP, scalar2=None, op0=ALU.add)
-        quantise_masks(0, 0)
-        quantise_masks(0, 1)
+        make_ep(0, 2, 2)
+        quantise_masks(0, 0, 0, 4)
+        quantise_masks(0, 1, 0, 4)
 
         compare(decr_t, th_lo, ALU.is_lt)
         compare(incr_t, th_hi, ALU.is_gt)
@@ -283,7 +287,7 @@ def tile_labelsmoothloss_pa_kernel(tc, predicts, adjList, label_prob_vec, out):
         transpose_p(8, 2)
         transpose_p(10, 2)
         nc.vector.tensor_tensor(out=incr_a_t[:, 0 : NC * L], in0=incr_t[:], in1=a_t[:], op=ALU.mult)
-        new_masks(4, 4)
+        new_masks(4)
         make_e(4, 4, 4)
         clear_diagonal(incr_a_t)
         transpose_back(incr_a_t, 0)
@@ -292,20 +296,19 @@ def tile_labelsmoothloss_pa_kernel(tc, predicts, adjList, label_prob_vec, out):
 
         make_ep(4, 4, 4)
         nc.vector.tensor_tensor(out=w_bf[2][:], in0=a_minus_1[:], in1=w_bf[1][:], op=ALU.mult)
-        quantise_masks(4, 0)
+        quantise_masks(4, 0, 4, 4)
         quantise_w(1)
-        quantise_masks(4, 1)
+        quantise_masks(4, 1, 4, 4)
         quantise_w(0)
-        new_masks(8, 8)
+        new_masks(8)
         make_e(8, 8, 8)
         quantise_w(2)
         make_ep(8, 8, 8)
-        quantise_masks(8, 0)
+        quantise_masks(8, 0, 8, 8)
 
         for r in range(EARLY_SIGNS):
             sign_pass(r)
-        row_factors(0)
-        quantise_masks(8, 1)
+        row_factors(0, lambda: quantise_masks(8, 1, 8, 4), lambda: quantise_masks(8, 1, 12, 4))
         for r in range(ON_GPSIMD):
             factor_pass(r)
         for r in range(EARLY_SIGNS, NT):
@@ -314,10 +317,14 @@ def tile_labelsmoothloss_pa_kernel(tc, predicts, adjList, label_prob_vec, out):
             factor_pass(r)
 
         run_of_adds(0)
-        row_factors(1)
+        row_factors(
+            1,
+            lambda: scale_and_store(nc.vector, ON_GPSIMD * L, L),
+            lambda: scale_and_store(nc.vector, (ON_GPSIMD + 1) * L, L),
+        )
         for r in range(STAT, NT):
             factor_pass(r)
-        for r in range(ON_GPSIMD, RUN):
+        for r in range(ON_GPSIMD + 2, RUN):
             scale_and_store(nc.vector, r * L, L)
         run_of_adds(RUN)
         scale_and_store(nc.vector, (RUN + ON_GPSIMD) * L, 2 * L)

@@ -22,9 +22,10 @@ PREDICT_LIMIT = 0.6
 RELATION_GAP = 0.05
 DIAG_STEP = L + P
 RUN = 8
-ON_GPSIMD = 3
-EARLY_SIGNS = 12
+STEEP = 2.0**64
+ON_VECTOR = (2, 4, 7, 9, 12, 15)
 STAT = NT // 2
+AHEAD = 5
 FLOPS = 3 * 2 * B * L * L
 
 
@@ -71,6 +72,8 @@ def tile_labelsmoothloss_pa_kernel(tc, predicts, adjList, label_prob_vec, out):
         make_identity(nc, ident[:])
         ident_b = keep.tile([P, P], BF16, name="ident_b")
         make_identity(nc, ident_b[:])
+        ones = keep.tile([P, 2], BF16, name="ones")
+        nc.gpsimd.memset(ones[:], 1.0)
         off_diag = keep.tile([P, P], BF16, name="off_diag")
         nc.vector.tensor_scalar(out=off_diag[:], in0=ident[:], scalar1=-1.0, scalar2=1.0, op0=ALU.mult, op1=ALU.add)
 
@@ -92,39 +95,22 @@ def tile_labelsmoothloss_pa_kernel(tc, predicts, adjList, label_prob_vec, out):
                 in_=bank[:, 0 : tiles * LW].rearrange("q (r u x) -> q r x u", r=tiles, u=2),
             )
 
-        mask_tiles = {}
+        e_t = keep.tile([P, NT * L], BF16, name="e_t", align_bytes=64)
+        ep_t = keep.tile([P, NT * L], BF16, name="ep_t", align_bytes=64)
 
-        def new_masks(first):
-            e_t = ring.tile([P, RUN * L], BF16, name="e_t", align_bytes=64)
-            ep_t = ring.tile([P, RUN * L], BF16, name="ep_t", align_bytes=64)
-            mask_tiles[first] = (e_t, ep_t)
+        def make_e(first, tiles):
+            c = slice(first * L, (first + tiles) * L)
+            nc.vector.tensor_scalar(out=e_t[:, c], in0=p_t[:, c], scalar1=PREDICT_LIMIT, scalar2=None, op0=ALU.is_gt)
 
-        def make_e(group, first, tiles):
-            c = slice((first - group) * L, (first - group + tiles) * L)
-            nc.vector.tensor_scalar(
-                out=mask_tiles[group][0][:, c],
-                in0=p_t[:, first * L : (first + tiles) * L],
-                scalar1=PREDICT_LIMIT,
-                scalar2=None,
-                op0=ALU.is_gt,
-            )
+        def make_ep(first, tiles):
+            c = slice(first * L, (first + tiles) * L)
+            nc.vector.tensor_tensor(out=ep_t[:, c], in0=e_t[:, c], in1=p_t[:, c], op=ALU.mult)
 
-        def make_ep(group, first, tiles):
-            c = slice((first - group) * L, (first - group + tiles) * L)
-            nc.vector.tensor_tensor(
-                out=mask_tiles[group][1][:, c],
-                in0=mask_tiles[group][0][:, c],
-                in1=p_t[:, first * L : (first + tiles) * L],
-                op=ALU.mult,
-            )
-
-        def quantise_masks(group, which, first, tiles):
-            codes, scales = ((e_codes, e_scales), (ep_codes, ep_scales))[which]
+        def quantise_masks(which, first, tiles):
+            codes, scales, src = ((e_codes, e_scales, e_t), (ep_codes, ep_scales, ep_t))[which]
             words = slice(first * P, (first + tiles) * P)
             nc.vector.quantize_mx(
-                out=codes[:, words].bitcast(FP8X4),
-                scales=scales[:, words],
-                in_=mask_tiles[group][which][:, (first - group) * L : (first - group + tiles) * L],
+                out=codes[:, words].bitcast(FP8X4), scales=scales[:, words], in_=src[:, first * L : (first + tiles) * L]
             )
 
         w_bf = [keep.tile([P, PACK * L], BF16, name="w_bf%d" % n, align_bytes=64) for n in range(3)]
@@ -183,44 +169,76 @@ def tile_labelsmoothloss_pa_kernel(tc, predicts, adjList, label_prob_vec, out):
                     in_=bank[:].rearrange("q (u j) -> q j u", u=2),
                 )
 
-        sgn = keep.tile([P, NT * L], BF16, name="sgn")
-        sgn_sum = keep.tile([P, NT], F32, name="sgn_sum")
-        twice_rel = keep.tile([P, 2 * NT], F32, name="twice_rel")
-        half_r = keep.tile([P, 2 * NT], F32, name="half_r")
-        step = keep.tile([P, NT], F32, name="step")
-        mid = keep.tile([P, NT], F32, name="mid")
+        e_words = e_t[:].bitcast(F32)
+        c_row = keep.tile([P, NT], F32, name="c_row")
+        den = keep.tile([P, NT], F32, name="den")
+        k_row = keep.tile([P, NT], F32, name="k_row")
+        ck_row = keep.tile([P, NT], F32, name="ck_row")
+        e_nat = keep.tile([P, NT * L], BF16, name="e_nat")
         factor = keep.tile([P, NT * L], F32, name="factor")
+        sum_banks = {}
+        e_banks = {}
 
-        def sign_pass(r):
+        def row_sums(batch):
+            bank = ps_a.tile([P, 2 * STAT], F32, name="sum_bank", tag="acc")
+            for k in range(STAT):
+                c0 = (batch * STAT + k) * L
+                for t in range(PACK):
+                    nc.tensor.matmul(
+                        bank[:, 2 * k : 2 * k + 2],
+                        lhsT=e_t[:, c0 + t : c0 + L : PACK],
+                        rhs=ones[:],
+                        start=(t == 0),
+                        stop=(t == PACK - 1),
+                    )
+            sum_banks[batch] = bank
+
+        def e_back(tiles):
+            bank = ps_t.tile([P, 2 * LW], F32, name="e_bank", tag="bank")
+            for k, r in enumerate(tiles):
+                for u in range(2):
+                    w0 = r * LW + u
+                    nc.tensor.transpose(
+                        bank[:, k * LW + u * P : k * LW + (u + 1) * P], e_words[:, w0 : w0 + LW - 1 : 2], ident[:]
+                    )
+                e_banks[r] = (bank, k)
+
+        def row_factors(batch, filler_1, filler_2, filler_3):
+            rows = slice(batch * STAT, (batch + 1) * STAT)
+            sums = sum_banks[batch][:, 0 : 2 * STAT : 2]
+            nc.vector.tensor_scalar(out=c_row[:, rows], in0=sums, scalar1=0.5, scalar2=None, op0=ALU.max)
+            filler_1()
+            nc.vector.scalar_tensor_tensor(
+                out=den[:, rows], in0=sums, scalar=1.0, in1=c_row[:, rows], op0=ALU.add, op1=ALU.mult
+            )
+            filler_2()
+            nc.vector.reciprocal(out=k_row[:, rows], in_=den[:, rows])
+            filler_3()
+            nc.vector.tensor_tensor(out=ck_row[:, rows], in0=c_row[:, rows], in1=k_row[:, rows], op=ALU.mult)
+
+        def e_natural(r):
             cols = slice(r * L, (r + 1) * L)
             nc.scalar.activation(
-                out=sgn[:, cols], in_=p_sb[:, cols], func=ACT.Sign, bias=-PREDICT_LIMIT, scale=1.0, accum_out=sgn_sum[:, r : r + 1]
+                out=e_nat[:, cols], in_=p_sb[:, cols], func=ACT.Sigmoid, bias=-PREDICT_LIMIT * STEEP, scale=STEEP
             )
-
-        def row_factors(batch, filler_1, filler_2):
-            rows = slice(batch * STAT, (batch + 1) * STAT)
-            both = slice(2 * batch * STAT, (2 * batch + 2) * STAT)
-            for_0 = slice(2 * batch * STAT, (2 * batch + 1) * STAT)
-            for_1 = slice((2 * batch + 1) * STAT, (2 * batch + 2) * STAT)
-            nc.vector.tensor_scalar(out=twice_rel[:, for_0], in0=sgn_sum[:, rows], scalar1=float(L + 2), scalar2=None, op0=ALU.add)
-            nc.vector.tensor_scalar(
-                out=twice_rel[:, for_1], in0=sgn_sum[:, rows], scalar1=float(L), scalar2=2.0, op0=ALU.add, op1=ALU.max
-            )
-            filler_1()
-            nc.vector.reciprocal(out=half_r[:, both], in_=twice_rel[:, both])
-            filler_2()
-            nc.vector.tensor_tensor(out=step[:, rows], in0=half_r[:, for_1], in1=half_r[:, for_0], op=ALU.subtract)
-            nc.vector.tensor_tensor(out=mid[:, rows], in0=half_r[:, for_1], in1=half_r[:, for_0], op=ALU.add)
 
         def factor_pass(r):
             cols = slice(r * L, (r + 1) * L)
-            nc.scalar.activation(
-                out=factor[:, cols], in_=sgn[:, cols], func=ACT.Identity, bias=mid[:, r : r + 1], scale=step[:, r : r + 1]
-            )
+            if r in ON_VECTOR:
+                nc.scalar.activation(out=factor[:, cols], in_=p_sb[:, cols], func=ACT.Identity, bias=0.0, scale=k_row[:, r : r + 1])
+            else:
+                nc.scalar.activation(
+                    out=factor[:, cols],
+                    in_=e_nat[:, cols],
+                    func=ACT.Identity,
+                    bias=ck_row[:, r : r + 1],
+                    scale=k_row[:, r : r + 1],
+                )
 
         num = keep.tile([P, RUN * L], F32, name="num")
+        accs = {}
 
-        def products_and_add(r):
+        def products(r):
             samples = slice(r * P, (r + 1) * P)
             acc = ps_a.tile([P, L], F32, name="acc", tag="acc")
             passes = ((ep_codes, ep_scales, 0), (e_codes, e_scales, 1), (ep_codes, ep_scales, 2))
@@ -234,24 +252,40 @@ def tile_labelsmoothloss_pa_kernel(tc, predicts, adjList, label_prob_vec, out):
                     start=(k == 0),
                     stop=(k == 2),
                 )
-            nc.vector.tensor_tensor(
-                out=num[:, (r % RUN) * L : (r % RUN + 1) * L], in0=acc[:], in1=p_sb[:, r * L : (r + 1) * L], op=ALU.add
-            )
+            accs[r] = acc
 
-        def scale_and_store(engine, c0, width):
-            n0 = c0 % (RUN * L)
-            if width > L:
-                res = ring.tile([P, 2 * L], F32, name="res_wide")
+        def num_of(r):
+            return num[:, (r % RUN) * L : (r % RUN + 1) * L]
+
+        def add_p(r):
+            if r in ON_VECTOR:
+                nc.vector.scalar_tensor_tensor(
+                    out=num_of(r),
+                    in0=accs[r][:],
+                    scalar=k_row[:, r : r + 1],
+                    in1=factor[:, r * L : (r + 1) * L],
+                    op0=ALU.mult,
+                    op1=ALU.add,
+                )
             else:
-                res = ring.tile([P, L], F32, name="res", bufs=8)
-            engine.tensor_tensor(out=res[:, 0:width], in0=num[:, n0 : n0 + width], in1=factor[:, c0 : c0 + width], op=ALU.mult)
-            nc.sync.dma_start(out=out_dram[:, c0 : c0 + width], in_=res[:, 0:width])
+                nc.vector.tensor_tensor(out=num_of(r), in0=accs[r][:], in1=p_sb[:, r * L : (r + 1) * L], op=ALU.add)
 
-        def run_of_adds(first):
-            for r in range(first, first + RUN):
-                products_and_add(r)
-                if r < first + ON_GPSIMD:
-                    scale_and_store(nc.gpsimd, r * L, L)
+        def finish(r, parts=1):
+            res = ring.tile([P, L], F32, name="res", bufs=10)
+            w = L // parts
+            for h in range(parts):
+                c = slice(h * w, (h + 1) * w)
+                if r in ON_VECTOR:
+                    bank, k = e_banks[r]
+                    e_ps = bank[:].bitcast(BF16)[:, k * L : (k + 1) * L]
+                    nc.vector.scalar_tensor_tensor(
+                        out=res[:, c], in0=e_ps[:, c], scalar=c_row[:, r : r + 1], in1=num_of(r)[:, c], op0=ALU.add, op1=ALU.mult
+                    )
+                else:
+                    nc.gpsimd.tensor_tensor(
+                        out=res[:, c], in0=num_of(r)[:, c], in1=factor[:, r * L + h * w : r * L + (h + 1) * w], op=ALU.mult
+                    )
+                nc.sync.dma_start(out=out_dram[:, r * L + h * w : r * L + (h + 1) * w], in_=res[:, c])
 
         transpose_p(0, 1)
         transpose_p(1, 1)
@@ -268,17 +302,16 @@ def tile_labelsmoothloss_pa_kernel(tc, predicts, adjList, label_prob_vec, out):
             scale=1.0,
         )
 
-        new_masks(0)
-        make_e(0, 0, 1)
-        make_e(0, 1, 1)
-        make_ep(0, 0, 1)
-        make_ep(0, 1, 1)
-        make_e(0, 2, 2)
+        make_e(0, 1)
+        make_e(1, 1)
+        make_ep(0, 1)
+        make_ep(1, 1)
+        make_e(2, 2)
         nc.vector.tensor_scalar(out=th_hi[:], in0=lp_t[:, 0:NC], scalar1=RELATION_GAP, scalar2=None, op0=ALU.add)
         nc.vector.tensor_scalar(out=th_lo[:], in0=lp_t[:, 0:NC], scalar1=-RELATION_GAP, scalar2=None, op0=ALU.add)
-        make_ep(0, 2, 2)
-        quantise_masks(0, 0, 0, 4)
-        quantise_masks(0, 1, 0, 4)
+        make_ep(2, 2)
+        quantise_masks(0, 0, 4)
+        quantise_masks(1, 0, 4)
 
         compare(decr_t, th_lo, ALU.is_lt)
         compare(incr_t, th_hi, ALU.is_gt)
@@ -287,47 +320,48 @@ def tile_labelsmoothloss_pa_kernel(tc, predicts, adjList, label_prob_vec, out):
         transpose_p(8, 2)
         transpose_p(10, 2)
         nc.vector.tensor_tensor(out=incr_a_t[:, 0 : NC * L], in0=incr_t[:], in1=a_t[:], op=ALU.mult)
-        new_masks(4)
-        make_e(4, 4, 4)
+        make_e(4, 4)
         clear_diagonal(incr_a_t)
         transpose_back(incr_a_t, 0)
         transpose_p(12, 2)
         transpose_p(14, 2)
+        row_sums(0)
+        e_back((2, 4))
 
-        make_ep(4, 4, 4)
+        make_ep(4, 4)
         nc.vector.tensor_tensor(out=w_bf[2][:], in0=a_minus_1[:], in1=w_bf[1][:], op=ALU.mult)
-        quantise_masks(4, 0, 4, 4)
+        quantise_masks(0, 4, 4)
         quantise_w(1)
-        quantise_masks(4, 1, 4, 4)
-        quantise_w(0)
-        new_masks(8)
-        make_e(8, 8, 8)
-        quantise_w(2)
-        make_ep(8, 8, 8)
-        quantise_masks(8, 0, 8, 8)
-
-        for r in range(EARLY_SIGNS):
-            sign_pass(r)
-        row_factors(0, lambda: quantise_masks(8, 1, 8, 4), lambda: quantise_masks(8, 1, 12, 4))
-        for r in range(ON_GPSIMD):
+        make_e(8, 8)
+        quantise_masks(1, 4, 4)
+        row_factors(0, lambda: quantise_w(0), lambda: quantise_w(2), lambda: quantise_masks(0, 8, 4))
+        for r in range(STAT):
+            if r not in ON_VECTOR:
+                e_natural(r)
+        for r in range(STAT):
             factor_pass(r)
-        for r in range(EARLY_SIGNS, NT):
-            sign_pass(r)
-        for r in range(ON_GPSIMD, STAT):
-            factor_pass(r)
-
-        run_of_adds(0)
+        row_sums(1)
+        e_back((7, 9))
+        for r in range(AHEAD):
+            products(r)
+        make_ep(8, 8)
         row_factors(
-            1,
-            lambda: scale_and_store(nc.vector, ON_GPSIMD * L, L),
-            lambda: scale_and_store(nc.vector, (ON_GPSIMD + 1) * L, L),
+            1, lambda: quantise_masks(0, 12, 4), lambda: quantise_masks(1, 8, 4), lambda: quantise_masks(1, 12, 4)
         )
         for r in range(STAT, NT):
+            if r not in ON_VECTOR:
+                e_natural(r)
+        for r in range(STAT, NT):
             factor_pass(r)
-        for r in range(ON_GPSIMD + 2, RUN):
-            scale_and_store(nc.vector, r * L, L)
-        run_of_adds(RUN)
-        scale_and_store(nc.vector, (RUN + ON_GPSIMD) * L, 2 * L)
-        scale_and_store(nc.vector, (RUN + ON_GPSIMD + 2) * L, 2 * L)
-        scale_and_store(nc.vector, (NT - 1) * L, L // 2)
-        scale_and_store(nc.vector, (NT - 1) * L + L // 2, L // 2)
+
+        for r in range(NT):
+            add_p(r)
+            if r + AHEAD < NT:
+                products(r + AHEAD)
+            if r not in ON_VECTOR:
+                finish(r)
+            if r - 1 in ON_VECTOR:
+                finish(r - 1)
+            if r == 6:
+                e_back((12, 15))
+        finish(NT - 1, 2)

@@ -23,7 +23,7 @@ RELATION_GAP = 0.05
 DIAG_STEP = L + P
 RUN = 8
 STEEP = 2.0**64
-ON_VECTOR = (2, 4, 7, 9, 12, 15)
+ON_VECTOR = (2, 4, 7, 9, 11, 13, 15)
 STAT = NT // 2
 AHEAD = 5
 FLOPS = 3 * 2 * B * L * L
@@ -78,33 +78,43 @@ def tile_labelsmoothloss_pa_kernel(tc, predicts, adjList, label_prob_vec, out):
         nc.vector.tensor_scalar(out=off_diag[:], in0=ident[:], scalar1=-1.0, scalar2=1.0, op0=ALU.mult, op1=ALU.add)
 
         p_words = p_sb[:].bitcast(F32)
-        p_t = keep.tile([P, NT * L], BF16, name="p_t", align_bytes=64)
-        p_t_words = p_t[:].bitcast(F32)
+        e_t = keep.tile([P, NT * L], BF16, name="e_t", align_bytes=64)
+        ep_t = keep.tile([P, NT * L], BF16, name="ep_t", align_bytes=64)
         e_codes = keep.tile([P, NT * P], U32, name="e_codes", align_bytes=64)
         e_scales = keep.tile([P, NT * P], U8, name="e_scales", align_bytes=64)
         ep_codes = keep.tile([P, NT * P], U32, name="ep_codes", align_bytes=64)
         ep_scales = keep.tile([P, NT * P], U8, name="ep_scales", align_bytes=64)
+        p_banks = {}
 
-        def transpose_p(first, tiles):
-            bank = ps_t.tile([P, 2 * LW], F32, name="bank")
-            for k in range(2 * tiles):
-                w0 = (first + k // 2) * LW + (k % 2) * P
-                nc.tensor.transpose(bank[:, k * P : (k + 1) * P], p_words[:, w0 : w0 + P], ident[:])
-            nc.scalar.copy(
-                out=p_t_words[:, first * LW : (first + tiles) * LW].rearrange("q (r x u) -> q r x u", r=tiles, u=2),
-                in_=bank[:, 0 : tiles * LW].rearrange("q (r u x) -> q r x u", r=tiles, u=2),
+        def transpose_p(first, tiles, pool, tag):
+            bank = pool.tile([P, 2 * LW], F32, name="p_bank", tag=tag)
+            half = tiles * P
+            for k in range(tiles):
+                for u in range(2):
+                    w0 = (first + k) * LW + u * P
+                    nc.tensor.transpose(bank[:, u * half + k * P : u * half + (k + 1) * P], p_words[:, w0 : w0 + P], ident[:])
+            view = bank[:].bitcast(BF16)[:, 0 : tiles * L].rearrange("q (u x e) -> q x u e", u=2, e=2)
+            p_banks[first] = (tiles, view)
+
+        def as_bank(m_t, first, tiles):
+            return m_t[:, first * L : (first + tiles) * L].rearrange("q (x u e) -> q x u e", u=2, e=2)
+
+        def make_e(engine, first):
+            tiles, bank = p_banks[first]
+            if engine is nc.vector:
+                engine.tensor_scalar(
+                    out=as_bank(e_t, first, tiles), in0=bank, scalar1=PREDICT_LIMIT, scalar2=None, op0=ALU.is_gt
+                )
+            else:
+                engine.activation(
+                    out=as_bank(e_t, first, tiles), in_=bank, func=ACT.Sigmoid, bias=-PREDICT_LIMIT * STEEP, scale=STEEP
+                )
+
+        def make_ep(first):
+            tiles, bank = p_banks[first]
+            nc.vector.tensor_tensor(
+                out=as_bank(ep_t, first, tiles), in0=as_bank(e_t, first, tiles), in1=bank, op=ALU.mult
             )
-
-        e_t = keep.tile([P, NT * L], BF16, name="e_t", align_bytes=64)
-        ep_t = keep.tile([P, NT * L], BF16, name="ep_t", align_bytes=64)
-
-        def make_e(first, tiles):
-            c = slice(first * L, (first + tiles) * L)
-            nc.vector.tensor_scalar(out=e_t[:, c], in0=p_t[:, c], scalar1=PREDICT_LIMIT, scalar2=None, op0=ALU.is_gt)
-
-        def make_ep(first, tiles):
-            c = slice(first * L, (first + tiles) * L)
-            nc.vector.tensor_tensor(out=ep_t[:, c], in0=e_t[:, c], in1=p_t[:, c], op=ALU.mult)
 
         def quantise_masks(which, first, tiles):
             codes, scales, src = ((e_codes, e_scales, e_t), (ep_codes, ep_scales, ep_t))[which]
@@ -127,6 +137,16 @@ def tile_labelsmoothloss_pa_kernel(tc, predicts, adjList, label_prob_vec, out):
         incr_a_t = keep.tile([P, NC * DIAG_STEP], BF16, name="incr_a_t")
         decr_t = keep.tile([P, NC * DIAG_STEP], BF16, name="decr_t")
         a_minus_1 = keep.tile([P, PACK * L], BF16, name="a_minus_1")
+
+        def subtract_1(side):
+            j = slice(side * 2 * P, (side + 1) * 2 * P)
+            nc.scalar.activation(
+                out=a_minus_1[:, side * 2 * P * PACK : (side + 1) * 2 * P * PACK].rearrange("q (j t) -> q j t", t=PACK),
+                in_=a_words[:].rearrange("q (t j) -> q j t", t=PACK)[:, j, :],
+                func=ACT.Identity,
+                bias=-1.0,
+                scale=1.0,
+            )
 
         def transpose_lp():
             lp_t = ps_a.tile([P, P], BF16, name="lp_t", tag="acc")
@@ -171,9 +191,8 @@ def tile_labelsmoothloss_pa_kernel(tc, predicts, adjList, label_prob_vec, out):
 
         e_words = e_t[:].bitcast(F32)
         c_row = keep.tile([P, NT], F32, name="c_row")
-        den = keep.tile([P, NT], F32, name="den")
-        k_row = keep.tile([P, NT], F32, name="k_row")
-        ck_row = keep.tile([P, NT], F32, name="ck_row")
+        den = keep.tile([P, 2 * NT], F32, name="den")
+        k_row = keep.tile([P, 2 * NT], F32, name="k_row")
         e_nat = keep.tile([P, NT * L], BF16, name="e_nat")
         factor = keep.tile([P, NT * L], F32, name="factor")
         sum_banks = {}
@@ -203,18 +222,29 @@ def tile_labelsmoothloss_pa_kernel(tc, predicts, adjList, label_prob_vec, out):
                     )
                 e_banks[r] = (bank, k)
 
-        def row_factors(batch, filler_1, filler_2, filler_3):
+        def row_factors(batch, filler_1, filler_2):
             rows = slice(batch * STAT, (batch + 1) * STAT)
+            first = 2 * batch * STAT
+            both = slice(first, first + 2 * STAT)
             sums = sum_banks[batch][:, 0 : 2 * STAT : 2]
             nc.vector.tensor_scalar(out=c_row[:, rows], in0=sums, scalar1=0.5, scalar2=None, op0=ALU.max)
+            nc.vector.tensor_scalar(
+                out=den[:, first + STAT : first + 2 * STAT], in0=sums, scalar1=1.0, scalar2=None, op0=ALU.add
+            )
             filler_1()
             nc.vector.scalar_tensor_tensor(
-                out=den[:, rows], in0=sums, scalar=1.0, in1=c_row[:, rows], op0=ALU.add, op1=ALU.mult
+                out=den[:, first : first + STAT], in0=sums, scalar=1.0, in1=c_row[:, rows], op0=ALU.add, op1=ALU.mult
             )
             filler_2()
-            nc.vector.reciprocal(out=k_row[:, rows], in_=den[:, rows])
-            filler_3()
-            nc.vector.tensor_tensor(out=ck_row[:, rows], in0=c_row[:, rows], in1=k_row[:, rows], op=ALU.mult)
+            nc.vector.reciprocal(out=k_row[:, both], in_=den[:, both])
+
+        def k_of(r):
+            c0 = 2 * (r // STAT) * STAT + r % STAT
+            return k_row[:, c0 : c0 + 1]
+
+        def ck_of(r):
+            c0 = (2 * (r // STAT) + 1) * STAT + r % STAT
+            return k_row[:, c0 : c0 + 1]
 
         def e_natural(r):
             cols = slice(r * L, (r + 1) * L)
@@ -225,14 +255,14 @@ def tile_labelsmoothloss_pa_kernel(tc, predicts, adjList, label_prob_vec, out):
         def factor_pass(r):
             cols = slice(r * L, (r + 1) * L)
             if r in ON_VECTOR:
-                nc.scalar.activation(out=factor[:, cols], in_=p_sb[:, cols], func=ACT.Identity, bias=0.0, scale=k_row[:, r : r + 1])
+                nc.scalar.activation(out=factor[:, cols], in_=p_sb[:, cols], func=ACT.Identity, bias=0.0, scale=k_of(r))
             else:
                 nc.scalar.activation(
                     out=factor[:, cols],
                     in_=e_nat[:, cols],
                     func=ACT.Identity,
-                    bias=ck_row[:, r : r + 1],
-                    scale=k_row[:, r : r + 1],
+                    bias=ck_of(r),
+                    scale=k_of(r),
                 )
 
         num = keep.tile([P, RUN * L], F32, name="num")
@@ -262,7 +292,7 @@ def tile_labelsmoothloss_pa_kernel(tc, predicts, adjList, label_prob_vec, out):
                 nc.vector.scalar_tensor_tensor(
                     out=num_of(r),
                     in0=accs[r][:],
-                    scalar=k_row[:, r : r + 1],
+                    scalar=k_of(r),
                     in1=factor[:, r * L : (r + 1) * L],
                     op0=ALU.mult,
                     op1=ALU.add,
@@ -287,74 +317,93 @@ def tile_labelsmoothloss_pa_kernel(tc, predicts, adjList, label_prob_vec, out):
                     )
                 nc.sync.dma_start(out=out_dram[:, r * L + h * w : r * L + (h + 1) * w], in_=res[:, c])
 
-        transpose_p(0, 1)
-        transpose_p(1, 1)
-        transpose_p(2, 2)
+        transpose_p(0, 1, ps_t, "bank")
+        transpose_p(1, 1, ps_t, "bank")
+        transpose_p(2, 1, ps_a, "acc")
+        transpose_p(3, 1, ps_a, "acc")
         lp_t = transpose_lp()
-        transpose_a()
-        transpose_p(4, 2)
-        transpose_p(6, 2)
-        nc.scalar.activation(
-            out=a_minus_1[:].rearrange("q (j t) -> q j t", t=PACK),
-            in_=a_words[:].rearrange("q (t j) -> q j t", t=PACK),
-            func=ACT.Identity,
-            bias=-1.0,
-            scale=1.0,
-        )
-
-        make_e(0, 1)
-        make_e(1, 1)
-        make_ep(0, 1)
-        make_ep(1, 1)
-        make_e(2, 2)
+        e_natural(0)
+        make_e(nc.scalar, 1)
+        make_e(nc.scalar, 3)
+        make_e(nc.vector, 0)
+        make_ep(0)
+        make_e(nc.vector, 2)
+        make_ep(1)
+        make_ep(2)
         nc.vector.tensor_scalar(out=th_hi[:], in0=lp_t[:, 0:NC], scalar1=RELATION_GAP, scalar2=None, op0=ALU.add)
         nc.vector.tensor_scalar(out=th_lo[:], in0=lp_t[:, 0:NC], scalar1=-RELATION_GAP, scalar2=None, op0=ALU.add)
-        make_ep(2, 2)
+        make_ep(3)
         quantise_masks(0, 0, 4)
         quantise_masks(1, 0, 4)
+        transpose_a()
+        transpose_p(4, 2, ps_t, "bank")
+        make_e(nc.scalar, 4)
+        transpose_p(6, 2, ps_t, "bank")
+        make_e(nc.scalar, 6)
 
         compare(decr_t, th_lo, ALU.is_lt)
-        compare(incr_t, th_hi, ALU.is_gt)
         clear_diagonal(decr_t)
+        subtract_1(0)
         transpose_back(decr_t, 1)
-        transpose_p(8, 2)
-        transpose_p(10, 2)
+        compare(incr_t, th_hi, ALU.is_gt)
+        make_ep(4)
         nc.vector.tensor_tensor(out=incr_a_t[:, 0 : NC * L], in0=incr_t[:], in1=a_t[:], op=ALU.mult)
-        make_e(4, 4)
+        make_ep(6)
         clear_diagonal(incr_a_t)
+        subtract_1(1)
         transpose_back(incr_a_t, 0)
-        transpose_p(12, 2)
-        transpose_p(14, 2)
+        transpose_p(8, 2, ps_a, "acc")
+        make_e(nc.scalar, 8)
+        transpose_p(10, 2, ps_a, "acc")
+        make_e(nc.scalar, 10)
         row_sums(0)
-        e_back((2, 4))
-
-        make_ep(4, 4)
-        nc.vector.tensor_tensor(out=w_bf[2][:], in0=a_minus_1[:], in1=w_bf[1][:], op=ALU.mult)
         quantise_masks(0, 4, 4)
-        quantise_w(1)
-        make_e(8, 8)
         quantise_masks(1, 4, 4)
-        row_factors(0, lambda: quantise_w(0), lambda: quantise_w(2), lambda: quantise_masks(0, 8, 4))
-        for r in range(STAT):
-            if r not in ON_VECTOR:
-                e_natural(r)
-        for r in range(STAT):
-            factor_pass(r)
-        row_sums(1)
-        e_back((7, 9))
-        for r in range(AHEAD):
+        quantise_w(1)
+        nc.vector.tensor_tensor(out=w_bf[2][:], in0=a_minus_1[:], in1=w_bf[1][:], op=ALU.mult)
+        quantise_w(0)
+        row_factors(0, lambda: quantise_w(2), lambda: make_ep(8))
+        transpose_p(12, 2, ps_t, "bank")
+        make_e(nc.scalar, 12)
+        transpose_p(14, 2, ps_t, "bank")
+        make_e(nc.scalar, 14)
+        for r in range(3):
             products(r)
-        make_ep(8, 8)
-        row_factors(
-            1, lambda: quantise_masks(0, 12, 4), lambda: quantise_masks(1, 8, 4), lambda: quantise_masks(1, 12, 4)
-        )
-        for r in range(STAT, NT):
-            if r not in ON_VECTOR:
-                e_natural(r)
-        for r in range(STAT, NT):
-            factor_pass(r)
+        make_ep(10)
+        quantise_masks(0, 8, 4)
+        quantise_masks(1, 8, 4)
 
-        for r in range(NT):
+        factor_pass(0)
+        e_natural(1)
+        factor_pass(2)
+        factor_pass(1)
+        e_natural(3)
+        factor_pass(4)
+        factor_pass(3)
+        e_natural(5)
+        e_natural(6)
+        factor_pass(5)
+        factor_pass(7)
+        factor_pass(6)
+        make_ep(12)
+        make_ep(14)
+        row_sums(1)
+        products(3)
+        e_back((2, 4))
+        quantise_masks(0, 12, 4)
+        quantise_masks(1, 12, 4)
+        row_factors(1, lambda: add_p(0), lambda: add_p(1))
+        finish(0)
+        finish(1)
+        products(4)
+        e_back((7, 9))
+        products(5)
+        products(6)
+        for r in range(STAT, NT, 2):
+            e_natural(r)
+            factor_pass(r + 1)
+            factor_pass(r)
+        for r in range(2, NT):
             add_p(r)
             if r + AHEAD < NT:
                 products(r + AHEAD)
@@ -363,5 +412,7 @@ def tile_labelsmoothloss_pa_kernel(tc, predicts, adjList, label_prob_vec, out):
             if r - 1 in ON_VECTOR:
                 finish(r - 1)
             if r == 6:
-                e_back((12, 15))
+                e_back((11, 13))
+            if r == 11:
+                e_back((15,))
         finish(NT - 1, 2)

@@ -88,16 +88,16 @@ def tile_labelsmoothloss_pa_kernel(tc, predicts, adjList, label_prob_vec, out):
 
         def transpose_p(first, tiles, pool, tag):
             bank = pool.tile([P, 2 * LW], F32, name="p_bank", tag=tag)
-            half = tiles * P
             for k in range(tiles):
                 for u in range(2):
                     w0 = (first + k) * LW + u * P
-                    nc.tensor.transpose(bank[:, u * half + k * P : u * half + (k + 1) * P], p_words[:, w0 : w0 + P], ident[:])
-            view = bank[:].bitcast(BF16)[:, 0 : tiles * L].rearrange("q (u x e) -> q x u e", u=2, e=2)
-            p_banks[first] = (tiles, view)
+                    nc.tensor.transpose(
+                        bank[:, k * LW + u : (k + 1) * LW - 1 + u : 2], p_words[:, w0 : w0 + P], ident[:]
+                    )
+            p_banks[first] = (tiles, bank[:].bitcast(BF16)[:, 0 : tiles * L])
 
         def as_bank(m_t, first, tiles):
-            return m_t[:, first * L : (first + tiles) * L].rearrange("q (x u e) -> q x u e", u=2, e=2)
+            return m_t[:, first * L : (first + tiles) * L]
 
         def make_e(engine, first):
             tiles, bank = p_banks[first]

@@ -72,6 +72,8 @@ def tile_labelsmoothloss_pa_kernel(tc, predicts, adjList, label_prob_vec, out):
         make_identity(nc, ident[:])
         ident_b = keep.tile([P, P], BF16, name="ident_b")
         make_identity(nc, ident_b[:])
+        zeros = keep.tile([P, L], BF16, name="zeros")
+        nc.vector.memset(zeros[:], 0.0)
         ones = keep.tile([P, 2], BF16, name="ones")
         nc.gpsimd.memset(ones[:], 1.0)
         off_diag = keep.tile([P, P], BF16, name="off_diag")
@@ -86,8 +88,13 @@ def tile_labelsmoothloss_pa_kernel(tc, predicts, adjList, label_prob_vec, out):
         ep_scales = keep.tile([P, NT * P], U8, name="ep_scales", align_bytes=64)
         p_banks = {}
 
-        def transpose_p(first, tiles, pool, tag):
+        def warm_up(bank, passes):
+            for i in range(passes):
+                nc.tensor.matmul(bank[:], lhsT=zeros[:, 0:P], rhs=zeros[:], start=True, stop=True)
+
+        def transpose_p(first, tiles, pool, tag, warm=0):
             bank = pool.tile([P, 2 * LW], F32, name="p_bank", tag=tag)
+            warm_up(bank, warm)
             for k in range(tiles):
                 for u in range(2):
                     w0 = (first + k) * LW + u * P
@@ -180,6 +187,8 @@ def tile_labelsmoothloss_pa_kernel(tc, predicts, adjList, label_prob_vec, out):
             dst = w_bf[n][:].bitcast(F32)
             for side in range(2):
                 bank = ps_a.tile([P, 2 * LW], F32, name="w_bank", tag="acc")
+                if side == 0:
+                    warm_up(bank, 3)
                 for k in range(2):
                     for u in range(2):
                         w0 = (2 * side + k) * LW + u * P
@@ -317,7 +326,7 @@ def tile_labelsmoothloss_pa_kernel(tc, predicts, adjList, label_prob_vec, out):
                     )
                 nc.sync.dma_start(out=out_dram[:, r * L + h * w : r * L + (h + 1) * w], in_=res[:, c])
 
-        transpose_p(0, 1, ps_t, "bank")
+        transpose_p(0, 1, ps_t, "bank", 3)
         transpose_p(1, 1, ps_t, "bank")
         transpose_p(2, 1, ps_a, "acc")
         transpose_p(3, 1, ps_a, "acc")
@@ -363,7 +372,7 @@ def tile_labelsmoothloss_pa_kernel(tc, predicts, adjList, label_prob_vec, out):
         nc.vector.tensor_tensor(out=w_bf[2][:], in0=a_minus_1[:], in1=w_bf[1][:], op=ALU.mult)
         quantise_w(0)
         row_factors(0, lambda: quantise_w(2), lambda: make_ep(8))
-        transpose_p(12, 2, ps_t, "bank")
+        transpose_p(12, 2, ps_t, "bank", 2)
         make_e(nc.scalar, 12)
         transpose_p(14, 2, ps_t, "bank")
         make_e(nc.scalar, 14)

@@ -35,7 +35,8 @@ def tile_labelsmoothloss_pa_kernel(tc, predicts, adjList, label_prob_vec, out):
         keep = ctx.enter_context(tc.tile_pool(name="keep", bufs=1))
         ring = ctx.enter_context(tc.tile_pool(name="ring", bufs=2))
         ps_t = ctx.enter_context(tc.psum_pool(name="ps_t", bufs=2))
-        ps_a = ctx.enter_context(tc.psum_pool(name="ps_a", bufs=6))
+        ps_e = ctx.enter_context(tc.psum_pool(name="ps_e", bufs=1))
+        ps_a = ctx.enter_context(tc.psum_pool(name="ps_a", bufs=5))
         ctx.enter_context(tc.manual_schedule())
 
         p_dram = predicts.rearrange("(x r) j -> x (r j)", r=NT)
@@ -173,8 +174,8 @@ def tile_labelsmoothloss_pa_kernel(tc, predicts, adjList, label_prob_vec, out):
                         )
                 nc.scalar.copy(out=a_t[:, side * 2 * L : (side + 1) * 2 * L], in_=bank[:])
 
-        def compare(dst, threshold, op):
-            for c in range(NC):
+        def compare(dst, threshold, op, first, blocks):
+            for c in range(first, first + blocks):
                 cols = slice(c * L, (c + 1) * L)
                 nc.vector.tensor_scalar(out=dst[:, cols], in0=a_t[:, cols], scalar1=threshold[:, c : c + 1], scalar2=None, op0=op)
 
@@ -188,7 +189,7 @@ def tile_labelsmoothloss_pa_kernel(tc, predicts, adjList, label_prob_vec, out):
             for side in range(2):
                 bank = ps_a.tile([P, 2 * LW], F32, name="w_bank", tag="acc")
                 if side == 0:
-                    warm_up(bank, 3)
+                    warm_up(bank, 2)
                 for k in range(2):
                     for u in range(2):
                         w0 = (2 * side + k) * LW + u * P
@@ -207,9 +208,12 @@ def tile_labelsmoothloss_pa_kernel(tc, predicts, adjList, label_prob_vec, out):
         sum_banks = {}
         e_banks = {}
 
-        def row_sums(batch):
-            bank = ps_a.tile([P, 2 * STAT], F32, name="sum_bank", tag="acc")
-            for k in range(STAT):
+        def row_sums(batch, first, tiles):
+            if first == 0:
+                bank = ps_a.tile([P, 2 * STAT], F32, name="sum_bank", tag="acc")
+            else:
+                bank = sum_banks[batch]
+            for k in range(first, first + tiles):
                 c0 = (batch * STAT + k) * L
                 for t in range(PACK):
                     nc.tensor.matmul(
@@ -221,8 +225,8 @@ def tile_labelsmoothloss_pa_kernel(tc, predicts, adjList, label_prob_vec, out):
                     )
             sum_banks[batch] = bank
 
-        def e_back(tiles):
-            bank = ps_t.tile([P, 2 * LW], F32, name="e_bank", tag="bank")
+        def e_back(tiles, pool, tag):
+            bank = pool.tile([P, 2 * LW], F32, name="e_bank", tag=tag)
             for k, r in enumerate(tiles):
                 for u in range(2):
                     w0 = r * LW + u
@@ -328,7 +332,7 @@ def tile_labelsmoothloss_pa_kernel(tc, predicts, adjList, label_prob_vec, out):
 
         transpose_p(0, 1, ps_t, "bank", 3)
         transpose_p(1, 1, ps_t, "bank")
-        transpose_p(2, 1, ps_a, "acc")
+        transpose_p(2, 1, ps_e, "e")
         transpose_p(3, 1, ps_a, "acc")
         lp_t = transpose_lp()
         e_natural(0)
@@ -349,39 +353,43 @@ def tile_labelsmoothloss_pa_kernel(tc, predicts, adjList, label_prob_vec, out):
         make_e(nc.scalar, 4)
         transpose_p(6, 2, ps_t, "bank")
         make_e(nc.scalar, 6)
-
-        compare(decr_t, th_lo, ALU.is_lt)
+        row_sums(0, 0, 4)
+        compare(decr_t, th_lo, ALU.is_lt, 0, 2)
+        compare(incr_t, th_hi, ALU.is_gt, 0, 2)
+        compare(decr_t, th_lo, ALU.is_lt, 2, 2)
+        compare(incr_t, th_hi, ALU.is_gt, 2, 1)
         clear_diagonal(decr_t)
         subtract_1(0)
         transpose_back(decr_t, 1)
-        compare(incr_t, th_hi, ALU.is_gt)
+        row_sums(0, 4, 4)
+        compare(incr_t, th_hi, ALU.is_gt, 3, 1)
         make_ep(4)
         nc.vector.tensor_tensor(out=incr_a_t[:, 0 : NC * L], in0=incr_t[:], in1=a_t[:], op=ALU.mult)
         make_ep(6)
         clear_diagonal(incr_a_t)
         subtract_1(1)
         transpose_back(incr_a_t, 0)
+        row_factors(0, lambda: quantise_masks(0, 4, 4), lambda: quantise_w(1))
         transpose_p(8, 2, ps_a, "acc")
         make_e(nc.scalar, 8)
         transpose_p(10, 2, ps_a, "acc")
         make_e(nc.scalar, 10)
-        row_sums(0)
-        quantise_masks(0, 4, 4)
+        e_back((2, 4), ps_e, "e")
         quantise_masks(1, 4, 4)
-        quantise_w(1)
         nc.vector.tensor_tensor(out=w_bf[2][:], in0=a_minus_1[:], in1=w_bf[1][:], op=ALU.mult)
         quantise_w(0)
-        row_factors(0, lambda: quantise_w(2), lambda: make_ep(8))
-        transpose_p(12, 2, ps_t, "bank", 2)
+        quantise_w(2)
+        transpose_p(12, 2, ps_t, "bank")
         make_e(nc.scalar, 12)
         transpose_p(14, 2, ps_t, "bank")
         make_e(nc.scalar, 14)
-        for r in range(3):
-            products(r)
+        make_ep(8)
         make_ep(10)
         quantise_masks(0, 8, 4)
         quantise_masks(1, 8, 4)
-
+        products(0)
+        row_sums(1, 0, 4)
+        products(1)
         factor_pass(0)
         e_natural(1)
         factor_pass(2)
@@ -396,32 +404,33 @@ def tile_labelsmoothloss_pa_kernel(tc, predicts, adjList, label_prob_vec, out):
         factor_pass(6)
         make_ep(12)
         make_ep(14)
-        row_sums(1)
+        row_sums(1, 4, 4)
+        products(2)
+        e_back((7, 9), ps_t, "bank")
         products(3)
-        e_back((2, 4))
         quantise_masks(0, 12, 4)
-        quantise_masks(1, 12, 4)
-        row_factors(1, lambda: add_p(0), lambda: add_p(1))
+        row_factors(1, lambda: quantise_masks(1, 12, 4), lambda: add_p(0))
+        add_p(1)
         finish(0)
         finish(1)
         products(4)
-        e_back((7, 9))
         products(5)
         products(6)
         for r in range(STAT, NT, 2):
             e_natural(r)
             factor_pass(r + 1)
             factor_pass(r)
-        for r in range(2, NT):
+        order = (0, 1, 2, 3, 4, 5, 6, 7, 8, 9, 10, 11, 12, 14, 13, 15)
+        for i, r in enumerate(order[2:], 2):
             add_p(r)
-            if r + AHEAD < NT:
-                products(r + AHEAD)
+            if i + AHEAD < NT:
+                products(order[i + AHEAD])
             if r not in ON_VECTOR:
                 finish(r)
-            if r - 1 in ON_VECTOR:
-                finish(r - 1)
-            if r == 6:
-                e_back((11, 13))
-            if r == 11:
-                e_back((15,))
-        finish(NT - 1, 2)
+            if order[i - 1] in ON_VECTOR:
+                finish(order[i - 1])
+            if i == 7:
+                e_back((11, 13), ps_t, "bank")
+            if i == 9:
+                e_back((15,), ps_e, "e")
+        finish(order[-1], 2)

@@ -23,7 +23,8 @@ RELATION_GAP = 0.05
 DIAG_STEP = L + P
 RUN = 8
 STEEP = 2.0**64
-ON_VECTOR = (2, 4, 7, 9, 11, 13, 15)
+ON_VECTOR = (2, 4, 7, 9, 11, 13)
+LAST = 15
 STAT = NT // 2
 AHEAD = 5
 FLOPS = 3 * 2 * B * L * L
@@ -283,7 +284,12 @@ def tile_labelsmoothloss_pa_kernel(tc, predicts, adjList, label_prob_vec, out):
 
         def products(r):
             samples = slice(r * P, (r + 1) * P)
-            acc = ps_a.tile([P, L], F32, name="acc", tag="acc")
+            if r == 4:
+                acc = ps_t.tile([P, L], F32, name="acc", tag="bank")
+            else:
+                acc = ps_a.tile([P, L], F32, name="acc", tag="acc")
+            if r == 0:
+                warm_up(acc, 2)
             passes = ((ep_codes, ep_scales, 0), (e_codes, e_scales, 1), (ep_codes, ep_scales, 2))
             for k, (codes, scales, n) in enumerate(passes):
                 nc.tensor.matmul_mx(
@@ -313,22 +319,24 @@ def tile_labelsmoothloss_pa_kernel(tc, predicts, adjList, label_prob_vec, out):
             else:
                 nc.vector.tensor_tensor(out=num_of(r), in0=accs[r][:], in1=p_sb[:, r * L : (r + 1) * L], op=ALU.add)
 
-        def finish(r, parts=1):
-            res = ring.tile([P, L], F32, name="res", bufs=10)
-            w = L // parts
-            for h in range(parts):
-                c = slice(h * w, (h + 1) * w)
-                if r in ON_VECTOR:
-                    bank, k = e_banks[r]
-                    e_ps = bank[:].bitcast(BF16)[:, k * L : (k + 1) * L]
-                    nc.vector.scalar_tensor_tensor(
-                        out=res[:, c], in0=e_ps[:, c], scalar=c_row[:, r : r + 1], in1=num_of(r)[:, c], op0=ALU.add, op1=ALU.mult
-                    )
-                else:
-                    nc.gpsimd.tensor_tensor(
-                        out=res[:, c], in0=num_of(r)[:, c], in1=factor[:, r * L + h * w : r * L + (h + 1) * w], op=ALU.mult
-                    )
-                nc.sync.dma_start(out=out_dram[:, r * L + h * w : r * L + (h + 1) * w], in_=res[:, c])
+        def finish(r, first=0, width=L, engine=None):
+            res = ring.tile([P, width], F32, name="res", tag="res%d" % width, bufs=10)
+            c = slice(first, first + width)
+            if r in ON_VECTOR:
+                bank, k = e_banks[r]
+                e_ps = bank[:].bitcast(BF16)[:, k * L : (k + 1) * L]
+                nc.vector.scalar_tensor_tensor(
+                    out=res[:], in0=e_ps[:, c], scalar=c_row[:, r : r + 1], in1=num_of(r)[:, c], op0=ALU.add, op1=ALU.mult
+                )
+            else:
+                engine.tensor_tensor(
+                    out=res[:], in0=num_of(r)[:, c], in1=factor[:, r * L + first : r * L + first + width], op=ALU.mult
+                )
+            return r, first, width, res
+
+        def store(part):
+            r, first, width, res = part
+            nc.sync.dma_start(out=out_dram[:, r * L + first : r * L + first + width], in_=res[:])
 
         transpose_p(0, 1, ps_t, "bank", 3)
         transpose_p(1, 1, ps_t, "bank")
@@ -404,33 +412,43 @@ def tile_labelsmoothloss_pa_kernel(tc, predicts, adjList, label_prob_vec, out):
         factor_pass(6)
         make_ep(12)
         make_ep(14)
-        row_sums(1, 4, 4)
         products(2)
+        row_sums(1, 4, 4)
         e_back((7, 9), ps_t, "bank")
         products(3)
+        products(4)
         quantise_masks(0, 12, 4)
         row_factors(1, lambda: quantise_masks(1, 12, 4), lambda: add_p(0))
         add_p(1)
-        finish(0)
-        finish(1)
-        products(4)
+        scaled = [(r, finish(r, engine=nc.gpsimd)) for r in range(2)]
         products(5)
         products(6)
         for r in range(STAT, NT, 2):
             e_natural(r)
-            factor_pass(r + 1)
-            factor_pass(r)
-        order = (0, 1, 2, 3, 4, 5, 6, 7, 8, 9, 10, 11, 12, 14, 13, 15)
+            if r + 1 == LAST:
+                factor_pass(r)
+                e_natural(LAST)
+                factor_pass(LAST)
+            else:
+                factor_pass(r + 1)
+                factor_pass(r)
+        order = (0, 1, 2, 3, 4, 5, 6, 7, 8, 9, 10, 11, 12, 13, 14, 15)
         for i, r in enumerate(order[2:], 2):
             add_p(r)
             if i + AHEAD < NT:
                 products(order[i + AHEAD])
-            if r not in ON_VECTOR:
-                finish(r)
             if order[i - 1] in ON_VECTOR:
-                finish(order[i - 1])
+                store(finish(order[i - 1]))
+            if r not in ON_VECTOR and r < 14:
+                scaled.append((i, finish(r, engine=nc.gpsimd)))
+            if r == 14:
+                scaled.append((i, finish(r, 0, 256, nc.gpsimd)))
+            if i >= scaled[0][0] + 2:
+                store(scaled.pop(0)[1])
             if i == 7:
-                e_back((11, 13), ps_t, "bank")
-            if i == 9:
-                e_back((15,), ps_e, "e")
-        finish(order[-1], 2)
+                e_back((11, 13), ps_e, "e")
+        for i, part in scaled:
+            store(part)
+        store(finish(14, 256, 256, nc.vector))
+        store(finish(15, 0, L // 2, nc.vector))
+        store(finish(15, L // 2, L // 2, nc.vector))

@@ -58,10 +58,11 @@ def tile_labelsmoothloss_pa_kernel(tc, predicts, adjList, label_prob_vec, out):
         load_p(0, 1)
         load_p(1, 1)
         load_p(2, 2)
-        nc.sync.dma_start(
-            out=a_rows[:].rearrange("p (c j) -> p c j", c=NC),
-            in_=adjList.rearrange("(c p) j -> p c j", p=P),
-        )
+        for half in range(2):
+            nc.sync.dma_start(
+                out=a_rows[:, half * 2 * L : (half + 1) * 2 * L].rearrange("p (c j) -> p c j", c=2),
+                in_=adjList[half * 2 * P : (half + 1) * 2 * P, :].rearrange("(c p) j -> p c j", p=P),
+            )
         load_p(4, 4)
         nc.sync.dma_start(
             out=a_words[:].rearrange("q (u w) -> q u w", u=2),
@@ -163,17 +164,19 @@ def tile_labelsmoothloss_pa_kernel(tc, predicts, adjList, label_prob_vec, out):
             return lp_t
 
         def transpose_a():
+            banks = [ps_a.tile([P, 2 * L], BF16, name="a_bank", tag="acc") for side in range(2)]
+            for half in range(2):
+                for side in range(2):
+                    for k in range(2):
+                        c = 2 * side + k
+                        for ci in range(2 * half, 2 * half + 2):
+                            nc.tensor.transpose(
+                                banks[side][:, k * L + ci * P : k * L + (ci + 1) * P],
+                                a_rows[:, ci * L + c * P : ci * L + (c + 1) * P],
+                                ident_b[:],
+                            )
             for side in range(2):
-                bank = ps_a.tile([P, 2 * L], BF16, name="a_bank", tag="acc")
-                for k in range(2):
-                    c = 2 * side + k
-                    for ci in range(NC):
-                        nc.tensor.transpose(
-                            bank[:, k * L + ci * P : k * L + (ci + 1) * P],
-                            a_rows[:, ci * L + c * P : ci * L + (c + 1) * P],
-                            ident_b[:],
-                        )
-                nc.scalar.copy(out=a_t[:, side * 2 * L : (side + 1) * 2 * L], in_=bank[:])
+                nc.scalar.copy(out=a_t[:, side * 2 * L : (side + 1) * 2 * L], in_=banks[side][:])
 
         def compare(dst, threshold, op, first, blocks):
             for c in range(first, first + blocks):
@@ -365,14 +368,13 @@ def tile_labelsmoothloss_pa_kernel(tc, predicts, adjList, label_prob_vec, out):
         compare(decr_t, th_lo, ALU.is_lt, 0, 2)
         compare(incr_t, th_hi, ALU.is_gt, 0, 2)
         compare(decr_t, th_lo, ALU.is_lt, 2, 2)
-        compare(incr_t, th_hi, ALU.is_gt, 2, 1)
+        compare(incr_t, th_hi, ALU.is_gt, 2, 2)
         clear_diagonal(decr_t)
         subtract_1(0)
         transpose_back(decr_t, 1)
         row_sums(0, 4, 4)
-        compare(incr_t, th_hi, ALU.is_gt, 3, 1)
-        make_ep(4)
         nc.vector.tensor_tensor(out=incr_a_t[:, 0 : NC * L], in0=incr_t[:], in1=a_t[:], op=ALU.mult)
+        make_ep(4)
         make_ep(6)
         clear_diagonal(incr_a_t)
         subtract_1(1)
@@ -450,5 +452,5 @@ def tile_labelsmoothloss_pa_kernel(tc, predicts, adjList, label_prob_vec, out):
         for i, part in scaled:
             store(part)
         store(finish(14, 256, 256, nc.vector))
-        store(finish(15, 0, L // 2, nc.vector))
-        store(finish(15, L // 2, L // 2, nc.vector))
+        store(finish(15, 0, 384, nc.vector))
+        store(finish(15, 384, 128, nc.vector))

@@ -23,8 +23,8 @@ RELATION_GAP = 0.05
 DIAG_STEP = L + P
 RUN = 8
 STEEP = 2.0**64
-ON_VECTOR = (2, 4, 7, 9, 11, 13)
-LAST = 15
+ON_VECTOR = (2, 4, 7, 9, 11, 13, 15)
+LAST = 99
 STAT = NT // 2
 AHEAD = 5
 FLOPS = 3 * 2 * B * L * L
@@ -420,37 +420,37 @@ def tile_labelsmoothloss_pa_kernel(tc, predicts, adjList, label_prob_vec, out):
         products(3)
         products(4)
         quantise_masks(0, 12, 4)
-        row_factors(1, lambda: quantise_masks(1, 12, 4), lambda: add_p(0))
+        row_factors(1, lambda: add_p(0), lambda: quantise_masks(1, 12, 4))
         add_p(1)
-        scaled = [(r, finish(r, engine=nc.gpsimd)) for r in range(2)]
+        scaled = [(r + 2, finish(r, engine=nc.gpsimd)) for r in range(2)]
         products(5)
         products(6)
         for r in range(STAT, NT, 2):
             e_natural(r)
-            if r + 1 == LAST:
-                factor_pass(r)
-                e_natural(LAST)
-                factor_pass(LAST)
-            else:
-                factor_pass(r + 1)
-                factor_pass(r)
+            factor_pass(r + 1)
+            factor_pass(r)
         order = (0, 1, 2, 3, 4, 5, 6, 7, 8, 9, 10, 11, 12, 13, 14, 15)
         for i, r in enumerate(order[2:], 2):
             add_p(r)
             if i + AHEAD < NT:
                 products(order[i + AHEAD])
+            while scaled and scaled[0][0] <= i:
+                store(scaled.pop(0)[1])
             if order[i - 1] in ON_VECTOR:
                 store(finish(order[i - 1]))
-            if r not in ON_VECTOR and r < 14:
-                scaled.append((i, finish(r, engine=nc.gpsimd)))
-            if r == 14:
-                scaled.append((i, finish(r, 0, 256, nc.gpsimd)))
-            if i >= scaled[0][0] + 2:
-                store(scaled.pop(0)[1])
+            if r not in ON_VECTOR:
+                if r in (12, 14):
+                    scaled.append((i + 2, finish(r, 0, 256, nc.gpsimd)))
+                    scaled.append((i + 2, finish(r, 256, 256, nc.gpsimd)))
+                else:
+                    scaled.append((i + 2, finish(r, engine=nc.gpsimd)))
             if i == 7:
                 e_back((11, 13), ps_e, "e")
-        for i, part in scaled:
+            if i == 11:
+                e_back((15,), ps_t, "bank")
+        parts = [part for due, part in scaled]
+        for part in parts[:-1]:
             store(part)
-        store(finish(14, 256, 256, nc.vector))
-        store(finish(15, 0, 384, nc.vector))
-        store(finish(15, 384, 128, nc.vector))
+        store(finish(15, 0, 256))
+        store(finish(15, 256, 256))
+        store(parts[-1])

@@ -309,18 +309,15 @@ def tile_labelsmoothloss_pa_kernel(tc, predicts, adjList, label_prob_vec, out):
         def num_of(r):
             return num[:, (r % RUN) * L : (r % RUN + 1) * L]
 
-        def add_p(r):
+        def add_p(r, first=0, width=L):
+            c = slice(first, first + width)
+            tile_c = slice(r * L + first, r * L + first + width)
             if r in ON_VECTOR:
                 nc.vector.scalar_tensor_tensor(
-                    out=num_of(r),
-                    in0=accs[r][:],
-                    scalar=k_of(r),
-                    in1=factor[:, r * L : (r + 1) * L],
-                    op0=ALU.mult,
-                    op1=ALU.add,
+                    out=num_of(r)[:, c], in0=accs[r][:, c], scalar=k_of(r), in1=factor[:, tile_c], op0=ALU.mult, op1=ALU.add
                 )
             else:
-                nc.vector.tensor_tensor(out=num_of(r), in0=accs[r][:], in1=p_sb[:, r * L : (r + 1) * L], op=ALU.add)
+                nc.vector.tensor_tensor(out=num_of(r)[:, c], in0=accs[r][:, c], in1=p_sb[:, tile_c], op=ALU.add)
 
         def finish(r, first=0, width=L, engine=None):
             res = ring.tile([P, width], F32, name="res", tag="res%d" % width, bufs=10)
@@ -394,8 +391,9 @@ def tile_labelsmoothloss_pa_kernel(tc, predicts, adjList, label_prob_vec, out):
         transpose_p(14, 2, ps_t, "bank")
         make_e(nc.scalar, 14)
         make_ep(8)
+        quantise_masks(0, 8, 2)
         make_ep(10)
-        quantise_masks(0, 8, 4)
+        quantise_masks(0, 10, 2)
         quantise_masks(1, 8, 4)
         products(0)
         row_sums(1, 0, 4)
@@ -431,7 +429,11 @@ def tile_labelsmoothloss_pa_kernel(tc, predicts, adjList, label_prob_vec, out):
             factor_pass(r)
         order = (0, 1, 2, 3, 4, 5, 6, 7, 8, 9, 10, 11, 12, 13, 14, 15)
         for i, r in enumerate(order[2:], 2):
-            add_p(r)
+            if r == 15:
+                add_p(r, 0, 256)
+                add_p(r, 256, 256)
+            else:
+                add_p(r)
             if i + AHEAD < NT:
                 products(order[i + AHEAD])
             while scaled and scaled[0][0] <= i:

@@ -57,13 +57,15 @@ def tile_labelsmoothloss_pa_kernel(tc, predicts, adjList, label_prob_vec, out):
         a_words = keep.tile([P, PACK * L], BF16, name="a_words")
         load_p(0, 1)
         load_p(1, 1)
-        load_p(2, 2)
+        load_p(2, 1)
+        load_p(3, 1)
         for half in range(2):
             nc.sync.dma_start(
                 out=a_rows[:, half * 2 * L : (half + 1) * 2 * L].rearrange("p (c j) -> p c j", c=2),
                 in_=adjList[half * 2 * P : (half + 1) * 2 * P, :].rearrange("(c p) j -> p c j", p=P),
             )
-        load_p(4, 4)
+        load_p(4, 2)
+        load_p(6, 2)
         nc.sync.dma_start(
             out=a_words[:].rearrange("q (u w) -> q u w", u=2),
             in_=adjList.rearrange("(u q e) j -> q u (e j)", u=2, e=2),

@@ -57,8 +57,7 @@ def tile_labelsmoothloss_pa_kernel(tc, predicts, adjList, label_prob_vec, out):
         a_words = keep.tile([P, PACK * L], BF16, name="a_words")
         load_p(0, 1)
         load_p(1, 1)
-        load_p(2, 1)
-        load_p(3, 1)
+        load_p(2, 2)
         for half in range(2):
             nc.sync.dma_start(
                 out=a_rows[:, half * 2 * L : (half + 1) * 2 * L].rearrange("p (c j) -> p c j", c=2),

from contextlib import ExitStack

import concourse.mybir as mybir
from concourse.masks import make_identity

F32 = mybir.dt.float32
BF16 = mybir.dt.bfloat16
U32 = mybir.dt.uint32
U8 = mybir.dt.uint8
FP8X4 = mybir.dt.float8_e4m3fn_x4
ALU = mybir.AluOpType
ACT = mybir.ActivationFunctionType

P = 128
B = 2048
L = 512
PACK = 4
LW = L // 2
NT = B // P
NC = L // P
PREDICT_LIMIT = 0.6
RELATION_GAP = 0.05
DIAG_STEP = L + P
RUN = 8
STEEP = 2.0**64
ON_VECTOR = (2, 4, 7, 9, 11, 13, 15)
LAST = 99
STAT = NT // 2
AHEAD = 5
FLOPS = 3 * 2 * B * L * L


def tile_labelsmoothloss_pa_kernel(tc, predicts, adjList, label_prob_vec, out):
    nc = tc.nc
    with ExitStack() as ctx:
        keep = ctx.enter_context(tc.tile_pool(name="keep", bufs=1))
        ring = ctx.enter_context(tc.tile_pool(name="ring", bufs=2))
        ps_t = ctx.enter_context(tc.psum_pool(name="ps_t", bufs=2))
        ps_e = ctx.enter_context(tc.psum_pool(name="ps_e", bufs=1))
        ps_a = ctx.enter_context(tc.psum_pool(name="ps_a", bufs=5))
        ctx.enter_context(tc.manual_schedule())

        p_dram = predicts.rearrange("(x r) j -> x (r j)", r=NT)
        out_dram = out.rearrange("(x r) j -> x (r j)", r=NT)

        lp_rows = keep.tile([P, P], BF16, name="lp_rows")
        nc.vector.memset(lp_rows[:], 0.0)
        nc.scalar.dma_start(out=lp_rows[0:NC, :], in_=label_prob_vec.rearrange("(c p) -> c p", p=P))

        p_sb = keep.tile([P, NT * L], BF16, name="p_sb")

        def load_p(first, tiles):
            cols = slice(first * L, (first + tiles) * L)
            nc.sync.dma_start(out=p_sb[:, cols], in_=p_dram[:, cols])

        a_rows = keep.tile([P, NC * L], BF16, name="a_rows")
        a_words = keep.tile([P, PACK * L], BF16, name="a_words")
        load_p(0, 1)
        load_p(1, 1)
        load_p(2, 2)
        for half in range(2):
            nc.sync.dma_start(
                out=a_rows[:, half * 2 * L : (half + 1) * 2 * L].rearrange("p (c j) -> p c j", c=2),
                in_=adjList[half * 2 * P : (half + 1) * 2 * P, :].rearrange("(c p) j -> p c j", p=P),
            )
        load_p(4, 2)
        load_p(6, 2)
        nc.sync.dma_start(
            out=a_words[:].rearrange("q (u w) -> q u w", u=2),
            in_=adjList.rearrange("(u q e) j -> q u (e j)", u=2, e=2),
        )
        load_p(8, 4)
        load_p(12, 4)

        ident = keep.tile([P, P], F32, name="ident")
        make_identity(nc, ident[:])
        ident_b = keep.tile([P, P], BF16, name="ident_b")
        make_identity(nc, ident_b[:])
        zeros = keep.tile([P, L], BF16, name="zeros")
        nc.vector.memset(zeros[:], 0.0)
        ones = keep.tile([P, 2], BF16, name="ones")
        nc.gpsimd.memset(ones[:], 1.0)
        off_diag = keep.tile([P, P], BF16, name="off_diag")
        nc.vector.tensor_scalar(out=off_diag[:], in0=ident[:], scalar1=-1.0, scalar2=1.0, op0=ALU.mult, op1=ALU.add)

        p_words = p_sb[:].bitcast(F32)
        e_t = keep.tile([P, NT * L], BF16, name="e_t", align_bytes=64)
        ep_t = keep.tile([P, NT * L], BF16, name="ep_t", align_bytes=64)
        e_codes = keep.tile([P, NT * P], U32, name="e_codes", align_bytes=64)
        e_scales = keep.tile([P, NT * P], U8, name="e_scales", align_bytes=64)
        ep_codes = keep.tile([P, NT * P], U32, name="ep_codes", align_bytes=64)
        ep_scales = keep.tile([P, NT * P], U8, name="ep_scales", align_bytes=64)
        p_banks = {}

        def warm_up(bank, passes):
            for i in range(passes):
                nc.tensor.matmul(bank[:], lhsT=zeros[:, 0:P], rhs=zeros[:], start=True, stop=True)

        def transpose_p(first, tiles, pool, tag, warm=0):
            bank = pool.tile([P, 2 * LW], F32, name="p_bank", tag=tag)
            warm_up(bank, warm)
            for k in range(tiles):
                for u in range(2):
                    w0 = (first + k) * LW + u * P
                    nc.tensor.transpose(
                        bank[:, k * LW + u : (k + 1) * LW - 1 + u : 2], p_words[:, w0 : w0 + P], ident[:]
                    )
            p_banks[first] = (tiles, bank[:].bitcast(BF16)[:, 0 : tiles * L])

        def as_bank(m_t, first, tiles):
            return m_t[:, first * L : (first + tiles) * L]

        def make_e(engine, first):
            tiles, bank = p_banks[first]
            if engine is nc.vector:
                engine.tensor_scalar(
                    out=as_bank(e_t, first, tiles), in0=bank, scalar1=PREDICT_LIMIT, scalar2=None, op0=ALU.is_gt
                )
            else:
                engine.activation(
                    out=as_bank(e_t, first, tiles), in_=bank, func=ACT.Sigmoid, bias=-PREDICT_LIMIT * STEEP, scale=STEEP
                )

        def make_ep(first):
            tiles, bank = p_banks[first]
            nc.vector.tensor_tensor(
                out=as_bank(ep_t, first, tiles), in0=as_bank(e_t, first, tiles), in1=bank, op=ALU.mult
            )

        def quantise_masks(which, first, tiles):
            codes, scales, src = ((e_codes, e_scales, e_t), (ep_codes, ep_scales, ep_t))[which]
            words = slice(first * P, (first + tiles) * P)
            nc.vector.quantize_mx(
                out=codes[:, words].bitcast(FP8X4), scales=scales[:, words], in_=src[:, first * L : (first + tiles) * L]
            )

        w_bf = [keep.tile([P, PACK * L], BF16, name="w_bf%d" % n, align_bytes=64) for n in range(3)]
        w_codes = [keep.tile([P, L], U32, name="w_codes%d" % n, align_bytes=64) for n in range(3)]
        w_scales = [keep.tile([P, L], U8, name="w_scales%d" % n, align_bytes=64) for n in range(3)]

        def quantise_w(n):
            nc.vector.quantize_mx(out=w_codes[n][:].bitcast(FP8X4), scales=w_scales[n][:], in_=w_bf[n][:])

        a_t = keep.tile([P, NC * L], BF16, name="a_t")
        th_hi = keep.tile([P, NC], F32, name="th_hi")
        th_lo = keep.tile([P, NC], F32, name="th_lo")
        incr_t = keep.tile([P, NC * L], BF16, name="incr_t")
        incr_a_t = keep.tile([P, NC * DIAG_STEP], BF16, name="incr_a_t")
        decr_t = keep.tile([P, NC * DIAG_STEP], BF16, name="decr_t")
        a_minus_1 = keep.tile([P, PACK * L], BF16, name="a_minus_1")

        def subtract_1(side):
            j = slice(side * 2 * P, (side + 1) * 2 * P)
            nc.scalar.activation(
                out=a_minus_1[:, side * 2 * P * PACK : (side + 1) * 2 * P * PACK].rearrange("q (j t) -> q j t", t=PACK),
                in_=a_words[:].rearrange("q (t j) -> q j t", t=PACK)[:, j, :],
                func=ACT.Identity,
                bias=-1.0,
                scale=1.0,
            )

        def transpose_lp():
            lp_t = ps_a.tile([P, P], BF16, name="lp_t", tag="acc")
            nc.tensor.transpose(lp_t[:], lp_rows[:], ident_b[:])
            return lp_t

        def transpose_a():
            banks = [ps_a.tile([P, 2 * L], BF16, name="a_bank", tag="acc") for side in range(2)]
            for half in range(2):
                for side in range(2):
                    for k in range(2):
                        c = 2 * side + k
                        for ci in range(2 * half, 2 * half + 2):
                            nc.tensor.transpose(
                                banks[side][:, k * L + ci * P : k * L + (ci + 1) * P],
                                a_rows[:, ci * L + c * P : ci * L + (c + 1) * P],
                                ident_b[:],
                            )
            for side in range(2):
                nc.scalar.copy(out=a_t[:, side * 2 * L : (side + 1) * 2 * L], in_=banks[side][:])

        def compare(dst, threshold, op, first, blocks):
            for c in range(first, first + blocks):
                cols = slice(c * L, (c + 1) * L)
                nc.vector.tensor_scalar(out=dst[:, cols], in0=a_t[:, cols], scalar1=threshold[:, c : c + 1], scalar2=None, op0=op)

        def clear_diagonal(m_t):
            blocks = m_t[:].rearrange("q (c w) -> q c w", w=DIAG_STEP)[:, :, 0:P]
            nc.vector.tensor_tensor(out=blocks, in0=blocks, in1=off_diag[:].unsqueeze(1).to_broadcast([P, NC, P]), op=ALU.mult)

        def transpose_back(m_t, n):
            src = m_t[:, 0 : NC * L].bitcast(F32)
            dst = w_bf[n][:].bitcast(F32)
            for side in range(2):
                bank = ps_a.tile([P, 2 * LW], F32, name="w_bank", tag="acc")
                if side == 0:
                    warm_up(bank, 2)
                for k in range(2):
                    for u in range(2):
                        w0 = (2 * side + k) * LW + u * P
                        nc.tensor.transpose(bank[:, u * LW + k * P : u * LW + (k + 1) * P], src[:, w0 : w0 + P], ident[:])
                nc.scalar.copy(
                    out=dst[:, side * 2 * LW : (side + 1) * 2 * LW].rearrange("q (j u) -> q j u", u=2),
                    in_=bank[:].rearrange("q (u j) -> q j u", u=2),
                )

        e_words = e_t[:].bitcast(F32)
        c_row = keep.tile([P, NT], F32, name="c_row")
        den = keep.tile([P, 2 * NT], F32, name="den")
        k_row = keep.tile([P, 2 * NT], F32, name="k_row")
        e_nat = keep.tile([P, NT * L], BF16, name="e_nat")
        factor = keep.tile([P, NT * L], F32, name="factor")
        sum_banks = {}
        e_banks = {}

        def row_sums(batch, first, tiles):
            if first == 0:
                bank = ps_a.tile([P, 2 * STAT], F32, name="sum_bank", tag="acc")
            else:
                bank = sum_banks[batch]
            for k in range(first, first + tiles):
                c0 = (batch * STAT + k) * L
                for t in range(PACK):
                    nc.tensor.matmul(
                        bank[:, 2 * k : 2 * k + 2],
                        lhsT=e_t[:, c0 + t : c0 + L : PACK],
                        rhs=ones[:],
                        start=(t == 0),
                        stop=(t == PACK - 1),
                    )
            sum_banks[batch] = bank

        def e_back(tiles, pool, tag):
            bank = pool.tile([P, 2 * LW], F32, name="e_bank", tag=tag)
            for k, r in enumerate(tiles):
                for u in range(2):
                    w0 = r * LW + u
                    nc.tensor.transpose(
                        bank[:, k * LW + u * P : k * LW + (u + 1) * P], e_words[:, w0 : w0 + LW - 1 : 2], ident[:]
                    )
                e_banks[r] = (bank, k)

        def row_factors(batch, filler_1, filler_2):
            rows = slice(batch * STAT, (batch + 1) * STAT)
            first = 2 * batch * STAT
            both = slice(first, first + 2 * STAT)
            sums = sum_banks[batch][:, 0 : 2 * STAT : 2]
            nc.vector.tensor_scalar(out=c_row[:, rows], in0=sums, scalar1=0.5, scalar2=None, op0=ALU.max)
            nc.vector.tensor_scalar(
                out=den[:, first + STAT : first + 2 * STAT], in0=sums, scalar1=1.0, scalar2=None, op0=ALU.add
            )
            filler_1()
            nc.vector.scalar_tensor_tensor(
                out=den[:, first : first + STAT], in0=sums, scalar=1.0, in1=c_row[:, rows], op0=ALU.add, op1=ALU.mult
            )
            filler_2()
            nc.vector.reciprocal(out=k_row[:, both], in_=den[:, both])

        def k_of(r):
            c0 = 2 * (r // STAT) * STAT + r % STAT
            return k_row[:, c0 : c0 + 1]

        def ck_of(r):
            c0 = (2 * (r // STAT) + 1) * STAT + r % STAT
            return k_row[:, c0 : c0 + 1]

        def e_natural(r):
            cols = slice(r * L, (r + 1) * L)
            nc.scalar.activation(
                out=e_nat[:, cols], in_=p_sb[:, cols], func=ACT.Sigmoid, bias=-PREDICT_LIMIT * STEEP, scale=STEEP
            )

        def factor_pass(r):
            cols = slice(r * L, (r + 1) * L)
            if r in ON_VECTOR:
                nc.scalar.activation(out=factor[:, cols], in_=p_sb[:, cols], func=ACT.Identity, bias=0.0, scale=k_of(r))
            else:
                nc.scalar.activation(
                    out=factor[:, cols],
                    in_=e_nat[:, cols],
                    func=ACT.Identity,
                    bias=ck_of(r),
                    scale=k_of(r),
                )

        num = keep.tile([P, RUN * L], F32, name="num")
        accs = {}

        def products(r):
            samples = slice(r * P, (r + 1) * P)
            if r == 4:
                acc = ps_t.tile([P, L], F32, name="acc", tag="bank")
            else:
                acc = ps_a.tile([P, L], F32, name="acc", tag="acc")
            if r == 0:
                warm_up(acc, 2)
            passes = ((ep_codes, ep_scales, 0), (e_codes, e_scales, 1), (ep_codes, ep_scales, 2))
            for k, (codes, scales, n) in enumerate(passes):
                nc.tensor.matmul_mx(
                    out=acc[:],
                    lhsT=codes[:, samples].bitcast(FP8X4),
                    lhsT_scale=scales[:, samples],
                    rhs=w_codes[n][:].bitcast(FP8X4),
                    rhs_scale=w_scales[n][:],
                    start=(k == 0),
                    stop=(k == 2),
                )
            accs[r] = acc

        def num_of(r):
            return num[:, (r % RUN) * L : (r % RUN + 1) * L]

        def add_p(r, first=0, width=L):
            c = slice(first, first + width)
            tile_c = slice(r * L + first, r * L + first + width)
            if r in ON_VECTOR:
                nc.vector.scalar_tensor_tensor(
                    out=num_of(r)[:, c], in0=accs[r][:, c], scalar=k_of(r), in1=factor[:, tile_c], op0=ALU.mult, op1=ALU.add
                )
            else:
                nc.vector.tensor_tensor(out=num_of(r)[:, c], in0=accs[r][:, c], in1=p_sb[:, tile_c], op=ALU.add)

        def finish(r, first=0, width=L, engine=None):
            res = ring.tile([P, width], F32, name="res", tag="res%d" % width, bufs=10)
            c = slice(first, first + width)
            if r in ON_VECTOR:
                bank, k = e_banks[r]
                e_ps = bank[:].bitcast(BF16)[:, k * L : (k + 1) * L]
                nc.vector.scalar_tensor_tensor(
                    out=res[:], in0=e_ps[:, c], scalar=c_row[:, r : r + 1], in1=num_of(r)[:, c], op0=ALU.add, op1=ALU.mult
                )
            else:
                engine.tensor_tensor(
                    out=res[:], in0=num_of(r)[:, c], in1=factor[:, r * L + first : r * L + first + width], op=ALU.mult
                )
            return r, first, width, res

        def store(part):
            r, first, width, res = part
            nc.sync.dma_start(out=out_dram[:, r * L + first : r * L + first + width], in_=res[:])

        transpose_p(0, 1, ps_t, "bank", 3)
        transpose_p(1, 1, ps_t, "bank")
        transpose_p(2, 1, ps_e, "e")
        transpose_p(3, 1, ps_a, "acc")
        lp_t = transpose_lp()
        e_natural(0)
        make_e(nc.scalar, 1)
        make_e(nc.scalar, 3)
        make_e(nc.vector, 0)
        make_ep(0)
        make_e(nc.vector, 2)
        make_ep(1)
        make_ep(2)
        nc.vector.tensor_scalar(out=th_hi[:], in0=lp_t[:, 0:NC], scalar1=RELATION_GAP, scalar2=None, op0=ALU.add)
        nc.vector.tensor_scalar(out=th_lo[:], in0=lp_t[:, 0:NC], scalar1=-RELATION_GAP, scalar2=None, op0=ALU.add)
        make_ep(3)
        quantise_masks(0, 0, 4)
        quantise_masks(1, 0, 4)
        transpose_a()
        transpose_p(4, 2, ps_t, "bank")
        make_e(nc.scalar, 4)
        transpose_p(6, 2, ps_t, "bank")
        make_e(nc.scalar, 6)
        row_sums(0, 0, 4)
        compare(decr_t, th_lo, ALU.is_lt, 0, 2)
        compare(incr_t, th_hi, ALU.is_gt, 0, 2)
        compare(decr_t, th_lo, ALU.is_lt, 2, 2)
        compare(incr_t, th_hi, ALU.is_gt, 2, 2)
        clear_diagonal(decr_t)
        subtract_1(0)
        transpose_back(decr_t, 1)
        row_sums(0, 4, 4)
        nc.vector.tensor_tensor(out=incr_a_t[:, 0 : NC * L], in0=incr_t[:], in1=a_t[:], op=ALU.mult)
        make_ep(4)
        make_ep(6)
        clear_diagonal(incr_a_t)
        subtract_1(1)
        transpose_back(incr_a_t, 0)
        row_factors(0, lambda: quantise_masks(0, 4, 4), lambda: quantise_w(1))
        transpose_p(8, 2, ps_a, "acc")
        make_e(nc.scalar, 8)
        transpose_p(10, 2, ps_a, "acc")
        make_e(nc.scalar, 10)
        e_back((2, 4), ps_e, "e")
        quantise_masks(1, 4, 4)
        nc.vector.tensor_tensor(out=w_bf[2][:], in0=a_minus_1[:], in1=w_bf[1][:], op=ALU.mult)
        quantise_w(0)
        quantise_w(2)
        transpose_p(12, 2, ps_t, "bank")
        make_e(nc.scalar, 12)
        transpose_p(14, 2, ps_t, "bank")
        make_e(nc.scalar, 14)
        make_ep(8)
        quantise_masks(0, 8, 2)
        make_ep(10)
        quantise_masks(0, 10, 2)
        quantise_masks(1, 8, 4)
        products(0)
        row_sums(1, 0, 4)
        products(1)
        factor_pass(0)
        e_natural(1)
        factor_pass(2)
        factor_pass(1)
        e_natural(3)
        factor_pass(4)
        factor_pass(3)
        e_natural(5)
        e_natural(6)
        factor_pass(5)
        factor_pass(7)
        factor_pass(6)
        make_ep(12)
        make_ep(14)
        products(2)
        row_sums(1, 4, 4)
        e_back((7, 9), ps_t, "bank")
        products(3)
        products(4)
        quantise_masks(0, 12, 4)
        row_factors(1, lambda: add_p(0), lambda: quantise_masks(1, 12, 4))
        add_p(1)
        scaled = [(r + 2, finish(r, engine=nc.gpsimd)) for r in range(2)]
        products(5)
        products(6)
        for r in range(STAT, NT, 2):
            e_natural(r)
            factor_pass(r + 1)
            factor_pass(r)
        order = (0, 1, 2, 3, 4, 5, 6, 7, 8, 9, 10, 11, 12, 13, 14, 15)
        for i, r in enumerate(order[2:], 2):
            if r == 15:
                add_p(r, 0, 256)
                add_p(r, 256, 256)
            else:
                add_p(r)
            if i + AHEAD < NT:
                products(order[i + AHEAD])
            while scaled and scaled[0][0] <= i:
                store(scaled.pop(0)[1])
            if order[i - 1] in ON_VECTOR:
                store(finish(order[i - 1]))
            if r not in ON_VECTOR:
                if r in (12, 14):
                    scaled.append((i + 2, finish(r, 0, 256, nc.gpsimd)))
                    scaled.append((i + 2, finish(r, 256, 256, nc.gpsimd)))
                else:
                    scaled.append((i + 2, finish(r, engine=nc.gpsimd)))
            if i == 7:
                e_back((11, 13), ps_e, "e")
            if i == 11:
                e_back((15,), ps_t, "bank")
        parts = [part for due, part in scaled]
        for part in parts[:-1]:
            store(part)
        store(finish(15, 0, 256))
        store(finish(15, 256, 256))
        store(parts[-1])
